import numpy as np
import ml_dtypes


def mxq(x, axis, fmt="e4m3"):
    dtype, down = {"e4m3": (ml_dtypes.float8_e4m3fn, 7), "e5m2": (ml_dtypes.float8_e5m2, 14)}[fmt]
    v = np.moveaxis(np.asarray(x, np.float32).astype(ml_dtypes.bfloat16).astype(np.float64), axis, -1)
    blocks = v.reshape(v.shape[:-1] + (-1, 32))
    amax = np.abs(blocks).max(-1, keepdims=True)
    byte = np.maximum(np.where(amax > 0, np.frexp(amax)[1] - 1 + 127, 0) - down, 1)
    scale = np.exp2(byte - 127.0)
    codes = (blocks / scale).astype(np.float32).astype(dtype).astype(np.float64)
    return np.moveaxis((codes * scale).reshape(v.shape), -1, axis)


WIDE = False


def mx_kscale(k):
    if not WIDE:
        return np.ones(k)
    levels = np.array([10, -10, 5, -5, 0])
    a = np.random.permutation(np.resize(levels, k // 512 * 4)).reshape(k // 512, 4)
    idx = np.arange(k)
    return np.exp2(a[idx // 512, idx % 128 // 32])


BF16 = ml_dtypes.bfloat16


def bf(x):
    return np.asarray(x, np.float32).astype(BF16)


def f64(x):
    return np.asarray(x).astype(np.float64)


E2M1 = np.array([0.0, 0.5, 1.0, 1.5, 2.0, 3.0, 4.0, 6.0, -0.0, -0.5, -1.0, -1.5, -2.0, -3.0, -4.0, -6.0])


def pack_weight(w, fmt):
    k, n = w.shape
    w = f64(bf(w)).reshape(k // 32, 32, n)
    amax = np.abs(w).max(1)
    if fmt == "e4m3":
        byte = np.frexp(amax)[1] - 1 + 127 - 7
    else:
        mant, ex = np.frexp(amax / 6.0)
        byte = np.where(mant > 0.5, ex, ex - 1) + 127
    byte = np.clip(np.where(amax > 0, byte, 1), 1, 254)
    scaled = (w * np.exp2(127.0 - byte)[:, None, :]).reshape(k, n).astype(np.float32)
    by_word = np.ascontiguousarray(scaled.reshape(k // 512, 128, 4, n).transpose(0, 1, 3, 2))
    if fmt == "e4m3":
        words = by_word.astype(ml_dtypes.float8_e4m3fn).view(np.uint8)
    else:
        c = by_word.astype(ml_dtypes.float4_e2m1fn).view(np.uint8) & 0xF
        words = c[..., 0::2] | (c[..., 1::2] << 4)
    return np.ascontiguousarray(words), np.ascontiguousarray(byte.astype(np.uint8).reshape(k // 512, 16, n))


def unpack_weight(words, scales, fmt):
    g, p, n, _ = words.shape
    if fmt == "e4m3":
        vals = np.ascontiguousarray(words).view(ml_dtypes.float8_e4m3fn).astype(np.float64)
    else:
        nib = np.empty((g, p, n, 4), np.uint8)
        nib[..., 0::2] = words & 0xF
        nib[..., 1::2] = words >> 4
        vals = E2M1[nib]
    vals = vals * np.repeat(np.exp2(scales.astype(np.float64) - 127.0), 8, axis=1)[..., None]
    return vals.transpose(0, 1, 3, 2).reshape(g * 512, n)


B, S, D, H, DN, DR, DV, RQ, RKV = 2, 64, 1024, 16, 64, 128, 128, 8192, 512
THETA = 10000.0
EPS = 1e-6
FMT = "e4m3"


def rmsnorm(v, w):
    return v * (1.0 / np.sqrt(np.mean(v * v, axis=-1, keepdims=True) + EPS)) * w


def rotate_half(v):
    v1 = v[..., ::2]
    v2 = v[..., 1::2]
    return np.stack((-v2, v1), axis=-1).reshape(v.shape)


def rope_cache():
    inv_freq = 1.0 / THETA ** (np.arange(0, DR, 2) / DR)
    freqs = np.outer(np.arange(S), inv_freq)
    emb = np.concatenate((freqs, freqs), -1)
    return np.cos(emb), np.sin(emb)


def apply_rope(v, cos, sin):
    return v * cos[None, None] + rotate_half(v) * sin[None, None]


def setup_inputs():
    s, t = mx_kscale(D), mx_kscale(RQ)
    x = bf(np.random.standard_normal((B, S, D)) * s)
    Wqa_words, Wqa_scales = pack_weight(np.random.standard_normal((D, RQ)) / np.sqrt(D) / s[:, None], FMT)
    q_a_norm_w = bf((1.0 + 0.1 * np.random.standard_normal(RQ)) * t)
    Wqb_words, Wqb_scales = pack_weight(np.random.standard_normal((RQ, H * (DN + DR))) / np.sqrt(RQ) / t[:, None], FMT)
    return {"x": x,
            "Wqa_words": Wqa_words,
            "Wqa_scales": Wqa_scales,
            "q_a_norm_w": q_a_norm_w,
            "Wqb_words": Wqb_words,
            "Wqb_scales": Wqb_scales}


def reference(x, Wqa_words, Wqa_scales, q_a_norm_w, Wqb_words, Wqb_scales):
    c = mxq(f64(x), 2, "e4m3") @ unpack_weight(Wqa_words, Wqa_scales, FMT)
    h = rmsnorm(c, f64(q_a_norm_w))
    q = mxq(h, 2, "e4m3") @ unpack_weight(Wqb_words, Wqb_scales, FMT)
    q = q.reshape(B, S, H, DN + DR).transpose(0, 2, 1, 3)
    q_nope, q_rope = q[..., :DN], q[..., DN:]
    cos, sin = rope_cache()
    q_rope = apply_rope(q_rope, cos, sin)
    return np.concatenate([q_nope, q_rope], -1)

@@ -1,0 +1,366 @@
+import math
+from contextlib import ExitStack
+
+import concourse.masks as masks
+import concourse.mybir as mybir
+
+F32 = mybir.dt.float32
+BF16 = mybir.dt.bfloat16
+I32 = mybir.dt.int32
+U32 = mybir.dt.uint32
+U8 = mybir.dt.uint8
+FP8X4 = mybir.dt.float8_e4m3fn_x4
+ALU = mybir.AluOpType
+ACT = mybir.ActivationFunctionType
+AXIS = mybir.AxisListType
+
+P = 128
+PACK = 4
+K_PASS = P * PACK
+BANK = 512
+
+BATCH, SEQ, D_MODEL = 2, 64, 1024
+RANK = 8192
+HEADS, D_NOPE, D_ROPE = 16, 64, 128
+D_HEAD = D_NOPE + D_ROPE
+THETA = 10000.0
+EPS = 1e-6
+
+X_PASSES = D_MODEL // K_PASS
+H_PASSES = RANK // K_PASS
+
+A_COLS = 2 * BANK
+A_PIECES = RANK // A_COLS
+PLANES = 4
+A_QUARTER = RANK // PLANES
+
+ROUNDS = 2
+ROUND_HEADS = HEADS // ROUNDS
+ROUND_COLS = ROUND_HEADS * D_HEAD
+ROUND_BANKS = ROUND_COLS // BANK
+B_PIECES = ROUNDS * H_PASSES
+B_AHEAD = 10
+
+ROUND_MAGIC = 12582912.0
+
+FLOPS = 2 * P * (D_MODEL * RANK + RANK * HEADS * D_HEAD)
+
+
+def tile_multiheadlatentattention_pa_k_kernel(
+    tc, x, Wqa_words, Wqa_scales, q_a_norm_w, Wqb_words, Wqb_scales, out
+):
+    nc = tc.nc
+    with ExitStack() as ctx:
+        keep = ctx.enter_context(tc.tile_pool(name="keep", bufs=1))
+        a_pool = ctx.enter_context(tc.tile_pool(name="a_pool", bufs=A_PIECES))
+        b_pool = ctx.enter_context(tc.tile_pool(name="b_pool", bufs=B_AHEAD))
+        stage = ctx.enter_context(tc.tile_pool(name="stage", bufs=4))
+        finish = ctx.enter_context(tc.tile_pool(name="finish", bufs=2))
+
+
+        a_planes = keep.tile([P, X_PASSES, A_QUARTER], U8, align_bytes=64)
+        b_planes = keep.tile([P, H_PASSES // PLANES, HEADS * D_HEAD], U8, align_bytes=64)
+        gain_rows = keep.tile([P, K_PASS], BF16)
+        nc.vector.memset(a_planes[:].rearrange("p g n -> p (g n)").bitcast(I32), 0)
+        nc.vector.memset(gain_rows[:], 0.0)
+        nc.vector.memset(b_planes[:].rearrange("p a n -> p (a n)").bitcast(I32), 0)
+
+        x_sb = keep.tile([P, D_MODEL], BF16)
+        for b in range(BATCH):
+            nc.sync.dma_start(out=x_sb[b:P:BATCH, :], in_=x[b])
+
+        nc.sync.dma_start(
+            out=gain_rows[0:H_PASSES, :],
+            in_=q_a_norm_w.rearrange("(g k) -> g k", g=H_PASSES),
+        )
+
+        for g in range(X_PASSES):
+            for quad in range(4):
+                nc.sync.dma_start(
+                    out=a_planes[32 * quad : 32 * quad + 16, g, :].bitcast(I32),
+                    in_=Wqa_scales[g, 4 * quad : 4 * quad + 4, :]
+                    .rearrange("r (j n) -> j r n", j=PLANES)
+                    .bitcast(I32),
+                )
+
+        a_words = Wqa_words.rearrange("g p n t -> p g (n t)")
+        a_pieces = []
+        for j in range(A_PIECES):
+            a_piece = a_pool.tile([P, X_PASSES, A_COLS], U32, align_bytes=64)
+            nc.sync.dma_start(
+                out=a_piece[:].bitcast(I32),
+                in_=a_words[:, :, PACK * A_COLS * j : PACK * A_COLS * (j + 1)].bitcast(I32),
+            )
+            a_pieces.append(a_piece)
+
+        for a in range(H_PASSES // PLANES):
+            for quad in range(4):
+                nc.sync.dma_start(
+                    out=b_planes[32 * quad : 32 * quad + 16, a, :].bitcast(I32),
+                    in_=Wqb_scales[
+                        PLANES * a : PLANES * (a + 1), 4 * quad : 4 * quad + 4, :
+                    ].bitcast(I32),
+                )
+
+        def load_b_piece(i):
+            rnd, g = divmod(i, H_PASSES)
+            b_piece = b_pool.tile([P, ROUND_COLS], U32, align_bytes=64)
+            nc.sync.dma_start(
+                out=b_piece[:].bitcast(I32),
+                in_=Wqb_words[g]
+                .rearrange("p n t -> p (n t)")[
+                    :, PACK * ROUND_COLS * rnd : PACK * ROUND_COLS * (rnd + 1)
+                ]
+                .bitcast(I32),
+            )
+            return b_piece
+
+        b_pieces = [load_b_piece(i) for i in range(B_AHEAD)]
+
+        ident = keep.tile([P, P], F32)
+        masks.make_identity(nc, ident[:])
+
+        angle_index = keep.tile([P, 2 * D_ROPE], I32)
+        nc.gpsimd.iota(
+            angle_index[:, 0:D_ROPE], pattern=[[0, 2], [1, 64]], base=0, channel_multiplier=0
+        )
+        nc.gpsimd.iota(
+            angle_index[:, D_ROPE : 2 * D_ROPE],
+            pattern=[[1, 2], [0, 2], [2, 32]],
+            base=0,
+            channel_multiplier=0,
+        )
+        partition_index = keep.tile([P, 1], I32)
+        nc.gpsimd.iota(partition_index[:], pattern=[[0, 1]], base=0, channel_multiplier=1)
+        position_int = keep.tile([P, 1], I32)
+        nc.vector.tensor_single_scalar(
+            out=position_int[:], in_=partition_index[:], scalar=1, op=ALU.arith_shift_right
+        )
+        position = keep.tile([P, 1], F32)
+        nc.vector.tensor_copy(out=position[:], in_=position_int[:])
+
+        inv_freq = keep.tile([P, 2 * D_ROPE], F32)
+        nc.vector.tensor_copy(out=inv_freq[:], in_=angle_index[:])
+        nc.scalar.activation(
+            out=inv_freq[:], in_=inv_freq[:], func=ACT.Exp, scale=-math.log(THETA) / 64.0
+        )
+        angle = keep.tile([P, 2 * D_ROPE], F32)
+        nc.vector.tensor_scalar(
+            out=angle[:, 0:D_ROPE],
+            in0=inv_freq[:, 0:D_ROPE],
+            scalar1=position[:, 0:1],
+            scalar2=math.pi / 2.0,
+            op0=ALU.mult,
+            op1=ALU.add,
+        )
+        nc.vector.tensor_scalar_mul(
+            out=angle[:, D_ROPE : 2 * D_ROPE],
+            in0=inv_freq[:, D_ROPE : 2 * D_ROPE],
+            scalar1=position[:, 0:1],
+        )
+        whole_turns = keep.tile([P, 2 * D_ROPE], F32)
+        nc.vector.tensor_scalar(
+            out=whole_turns[:],
+            in0=angle[:],
+            scalar1=1.0 / (2.0 * math.pi),
+            scalar2=ROUND_MAGIC,
+            op0=ALU.mult,
+            op1=ALU.add,
+        )
+        nc.vector.tensor_scalar(
+            out=whole_turns[:],
+            in0=whole_turns[:],
+            scalar1=ROUND_MAGIC,
+            scalar2=2.0 * math.pi,
+            op0=ALU.subtract,
+            op1=ALU.mult,
+        )
+        nc.vector.tensor_sub(out=angle[:], in0=angle[:], in1=whole_turns[:])
+        table = keep.tile([P, 2 * D_ROPE], F32)
+        nc.scalar.activation(out=table[:], in_=angle[:], func=ACT.Sin)
+        cos_table = table[:, 0:D_ROPE]
+        sin_planes = table[:, D_ROPE : 2 * D_ROPE].rearrange("p (two i) -> p two i", two=2)
+        nc.vector.tensor_scalar_mul(
+            out=sin_planes[:, 0, :], in0=sin_planes[:, 0, :], scalar1=-1.0
+        )
+
+        square_sums = keep.tile([P, H_PASSES], F32)
+        c_gain = keep.tile([P, H_PASSES, P, PACK], F32)
+        rstd_all = keep.tile([P, P], F32)
+
+        with tc.psum_pool(name="psum_c", bufs=4) as psum_c:
+            x_words = x_sb[:].bitcast(F32)
+            x_t = psum_c.tile([P, X_PASSES, 2, P], F32, tag="transposed")
+            for g in range(X_PASSES):
+                for u in range(2):
+                    nc.tensor.transpose(
+                        x_t[:, g, u, :],
+                        x_words[:, 256 * g + u : 256 * (g + 1) : 2],
+                        ident[:],
+                    )
+            x_grouped = keep.tile([P, X_PASSES * P * PACK], BF16, align_bytes=64)
+            nc.vector.tensor_copy(
+                out=x_grouped[:].bitcast(F32).rearrange("p (g k u) -> p g k u", g=X_PASSES, u=2),
+                in_=x_t[:].rearrange("p g u k -> p g k u"),
+            )
+            x_codes = keep.tile([P, X_PASSES * P], U32, align_bytes=64)
+            x_scales = keep.tile([P, X_PASSES * P], U8, align_bytes=64)
+            nc.vector.quantize_mx(
+                out=x_codes[:].bitcast(FP8X4), scales=x_scales[:], in_=x_grouped[:]
+            )
+
+            gain_sorted = keep.tile([P, PACK, P], F32)
+            nc.vector.tensor_copy(
+                out=gain_sorted[:], in_=gain_rows[:].rearrange("g (p t) -> g t p", t=PACK)
+            )
+            gain_t = psum_c.tile([P, PACK, P], F32, tag="transposed")
+            for t in range(PACK):
+                nc.tensor.transpose(gain_t[:, t, :], gain_sorted[:, t, :], ident[:])
+            gain = keep.tile([P, H_PASSES, PACK], F32)
+            nc.vector.tensor_copy(
+                out=gain[:], in_=gain_t[:, :, 0:H_PASSES].rearrange("p t g -> p g t")
+            )
+
+            def multiply_piece(j):
+                sorted_banks = []
+                for half in range(A_COLS // BANK):
+                    g = (A_COLS // BANK) * j + half
+                    plane, plane_col = divmod(BANK * g, A_QUARTER)
+                    c_bank = psum_c.tile([P, BANK], F32, tag="c_bank")
+                    for xg in range(X_PASSES):
+                        nc.tensor.matmul_mx(
+                            out=c_bank[:],
+                            lhsT=x_codes[:, P * xg : P * (xg + 1)].bitcast(FP8X4),
+                            lhsT_scale=x_scales[:, P * xg : P * (xg + 1)],
+                            rhs=a_pieces[j][:, xg, BANK * half : BANK * (half + 1)].bitcast(FP8X4),
+                            rhs_scale=a_planes[4 * plane : P, xg, plane_col : plane_col + BANK],
+                            start=(xg == 0),
+                            stop=(xg == X_PASSES - 1),
+                        )
+                    c_sorted = stage.tile([P, PACK, P], F32)
+                    nc.scalar.copy(
+                        out=c_sorted[:], in_=c_bank[:].rearrange("k (p t) -> k t p", t=PACK)
+                    )
+                    squares = stage.tile([P, BANK], BF16, bufs=2)
+                    nc.scalar.activation(
+                        out=squares[:],
+                        in_=c_bank[:],
+                        func=ACT.Square,
+                        accum_out=square_sums[:, g : g + 1],
+                    )
+                    sorted_banks.append((g, c_sorted))
+                return sorted_banks
+
+            def transpose_piece(sorted_banks):
+                for g, c_sorted in sorted_banks:
+                    c_t = psum_c.tile([P, PACK, P], F32, tag="transposed")
+                    for t in range(PACK):
+                        nc.tensor.transpose(c_t[:, t, :], c_sorted[:, t, :], ident[:])
+                    nc.vector.tensor_tensor(
+                        out=c_gain[:, g, :, :],
+                        in0=c_t[:].rearrange("p t k -> p k t"),
+                        in1=gain[:, g, :].unsqueeze(1).to_broadcast([P, P, PACK]),
+                        op=ALU.mult,
+                    )
+
+            waiting = multiply_piece(0)
+            for j in range(1, A_PIECES):
+                arrived = multiply_piece(j)
+                transpose_piece(waiting)
+                waiting = arrived
+            transpose_piece(waiting)
+
+            mean_square = keep.tile([P, 1], F32)
+            nc.vector.reduce_sum(out=mean_square[:], in_=square_sums[:], axis=AXIS.X)
+            nc.vector.tensor_scalar(
+                out=mean_square[:],
+                in0=mean_square[:],
+                scalar1=1.0 / RANK,
+                scalar2=EPS,
+                op0=ALU.mult,
+                op1=ALU.add,
+            )
+            rstd = keep.tile([P, 1], F32)
+            nc.scalar.sqrt(out=rstd[:], in_=mean_square[:])
+            nc.vector.reciprocal(out=rstd[:], in_=rstd[:])
+            rstd_t = psum_c.tile([P, P], F32, tag="transposed")
+            nc.tensor.transpose(rstd_t[:], rstd[:, 0:1].to_broadcast([P, P]), ident[:])
+            nc.vector.tensor_copy(out=rstd_all[:], in_=rstd_t[:])
+
+        h_codes = keep.tile([P, H_PASSES, P], U32, align_bytes=64)
+        h_scales = keep.tile([P, H_PASSES, P], U8, align_bytes=64)
+        for g in range(H_PASSES):
+            h_grouped = stage.tile([P, P, PACK], BF16, align_bytes=64)
+            nc.vector.tensor_tensor(
+                out=h_grouped[:],
+                in0=c_gain[:, g, :, :],
+                in1=rstd_all[:].unsqueeze(2).to_broadcast([P, P, PACK]),
+                op=ALU.mult,
+            )
+            nc.vector.quantize_mx(
+                out=h_codes[:, g, :].bitcast(FP8X4),
+                scales=h_scales[:, g, :],
+                in_=h_grouped[:].rearrange("p k t -> p (k t)"),
+            )
+
+        with tc.psum_pool(name="psum_q", bufs=ROUNDS) as psum_q:
+            for rnd in range(ROUNDS):
+                q_banks = []
+                for bank in range(ROUND_BANKS):
+                    q_bank = psum_q.tile([P, BANK], F32, tag="q_bank%d" % bank)
+                    q_banks.append(q_bank)
+                for g in range(H_PASSES):
+                    i = H_PASSES * rnd + g
+                    a, plane = divmod(g, PLANES)
+                    for bank in range(ROUND_BANKS):
+                        col = ROUND_COLS * rnd + BANK * bank
+                        nc.tensor.matmul_mx(
+                            out=q_banks[bank][:],
+                            lhsT=h_codes[:, g, :].bitcast(FP8X4),
+                            lhsT_scale=h_scales[:, g, :],
+                            rhs=b_pieces[i][:, BANK * bank : BANK * (bank + 1)].bitcast(FP8X4),
+                            rhs_scale=b_planes[4 * plane : P, a, col : col + BANK],
+                            start=(g == 0),
+                            stop=(g == H_PASSES - 1),
+                        )
+                    if i + B_AHEAD < B_PIECES:
+                        b_pieces.append(load_b_piece(i + B_AHEAD))
+
+                q_heads = finish.tile([P, ROUND_HEADS, D_HEAD], F32)
+                q_flat = q_heads[:].rearrange("p h f -> p (h f)")
+                for bank in range(ROUND_BANKS):
+                    nc.scalar.copy(
+                        out=q_flat[:, BANK * bank : BANK * (bank + 1)], in_=q_banks[bank][:]
+                    )
+                rope = q_heads[:, :, D_NOPE:D_HEAD]
+                pairs = rope.rearrange("p h (i two) -> p h i two", two=2)
+                neighbour = finish.tile([P, ROUND_HEADS, 2, D_ROPE // 2], F32, bufs=1)
+                for two in range(2):
+                    nc.vector.tensor_tensor(
+                        out=neighbour[:, :, two, :],
+                        in0=pairs[:, :, :, 1 - two],
+                        in1=sin_planes[:, two, :]
+                        .unsqueeze(1)
+                        .to_broadcast([P, ROUND_HEADS, D_ROPE // 2]),
+                        op=ALU.mult,
+                    )
+                nc.vector.tensor_tensor(
+                    out=rope,
+                    in0=rope,
+                    in1=cos_table.unsqueeze(1).to_broadcast([P, ROUND_HEADS, D_ROPE]),
+                    op=ALU.mult,
+                )
+                nc.vector.tensor_tensor(
+                    out=pairs,
+                    in0=pairs,
+                    in1=neighbour[:].rearrange("p h two i -> p h i two"),
+                    op=ALU.add,
+                )
+                store_queue = nc.sync if rnd == ROUNDS - 1 else nc.scalar
+                for b in range(BATCH):
+                    store_queue.dma_start(
+                        out=out[b, ROUND_HEADS * rnd : ROUND_HEADS * (rnd + 1)].rearrange(
+                            "h s f -> s h f"
+                        ),
+                        in_=q_heads[b:P:BATCH, :, :],
+                    )

@@ -34,16 +34,26 @@ A_PIECES = RANK // A_COLS
 PLANES = 4
 A_QUARTER = RANK // PLANES
 
-ROUNDS = 2
-ROUND_HEADS = HEADS // ROUNDS
-ROUND_COLS = ROUND_HEADS * D_HEAD
-ROUND_BANKS = ROUND_COLS // BANK
+LAST_ROUND_HEADS = 4
+ROUND_HEADS = (HEADS - LAST_ROUND_HEADS, LAST_ROUND_HEADS)
+ROUNDS = len(ROUND_HEADS)
 B_PIECES = ROUNDS * H_PASSES
-B_AHEAD = 10
+B_AHEAD = 6
 
 ROUND_MAGIC = 12582912.0
 
 FLOPS = 2 * P * (D_MODEL * RANK + RANK * HEADS * D_HEAD)
+
+
+def moving_slices(cols):
+    slices = []
+    start = 0
+    for width in (BANK, 256, 128):
+        while cols - start >= width:
+            slices.append((start, width))
+            start += width
+    assert start == cols
+    return slices
 
 
 def tile_multiheadlatentattention_pa_k_kernel(
@@ -55,7 +65,7 @@ def tile_multiheadlatentattention_pa_k_kernel(
         a_pool = ctx.enter_context(tc.tile_pool(name="a_pool", bufs=A_PIECES))
         b_pool = ctx.enter_context(tc.tile_pool(name="b_pool", bufs=B_AHEAD))
         stage = ctx.enter_context(tc.tile_pool(name="stage", bufs=4))
-        finish = ctx.enter_context(tc.tile_pool(name="finish", bufs=2))
+        finish = ctx.enter_context(tc.tile_pool(name="finish", bufs=1))
 
 
         a_planes = keep.tile([P, X_PASSES, A_QUARTER], U8, align_bytes=64)
@@ -102,15 +112,17 @@ def tile_multiheadlatentattention_pa_k_kernel(
                     ].bitcast(I32),
                 )
 
+        first_head = [sum(ROUND_HEADS[:rnd]) for rnd in range(ROUNDS)]
+
         def load_b_piece(i):
             rnd, g = divmod(i, H_PASSES)
-            b_piece = b_pool.tile([P, ROUND_COLS], U32, align_bytes=64)
+            first_col = first_head[rnd] * D_HEAD
+            cols = ROUND_HEADS[rnd] * D_HEAD
+            b_piece = b_pool.tile([P, cols], U32, align_bytes=64)
             nc.sync.dma_start(
                 out=b_piece[:].bitcast(I32),
                 in_=Wqb_words[g]
-                .rearrange("p n t -> p (n t)")[
-                    :, PACK * ROUND_COLS * rnd : PACK * ROUND_COLS * (rnd + 1)
-                ]
+                .rearrange("p n t -> p (n t)")[:, PACK * first_col : PACK * (first_col + cols)]
                 .bitcast(I32),
             )
             return b_piece
@@ -303,51 +315,52 @@ def tile_multiheadlatentattention_pa_k_kernel(
                 in_=h_grouped[:].rearrange("p k t -> p (k t)"),
             )
 
-        with tc.psum_pool(name="psum_q", bufs=ROUNDS) as psum_q:
+        with tc.psum_pool(name="psum_q", bufs=1) as psum_q:
             for rnd in range(ROUNDS):
+                heads = ROUND_HEADS[rnd]
+                first_col = first_head[rnd] * D_HEAD
+                slices = moving_slices(heads * D_HEAD)
                 q_banks = []
-                for bank in range(ROUND_BANKS):
-                    q_bank = psum_q.tile([P, BANK], F32, tag="q_bank%d" % bank)
+                for n, (start, width) in enumerate(slices):
+                    q_bank = psum_q.tile([P, width], F32, tag="q_bank_%d_%d" % (rnd, n))
                     q_banks.append(q_bank)
                 for g in range(H_PASSES):
                     i = H_PASSES * rnd + g
                     a, plane = divmod(g, PLANES)
-                    for bank in range(ROUND_BANKS):
-                        col = ROUND_COLS * rnd + BANK * bank
+                    for q_bank, (start, width) in zip(q_banks, slices):
+                        col = first_col + start
                         nc.tensor.matmul_mx(
-                            out=q_banks[bank][:],
+                            out=q_bank[:],
                             lhsT=h_codes[:, g, :].bitcast(FP8X4),
                             lhsT_scale=h_scales[:, g, :],
-                            rhs=b_pieces[i][:, BANK * bank : BANK * (bank + 1)].bitcast(FP8X4),
-                            rhs_scale=b_planes[4 * plane : P, a, col : col + BANK],
+                            rhs=b_pieces[i][:, start : start + width].bitcast(FP8X4),
+                            rhs_scale=b_planes[4 * plane : P, a, col : col + width],
                             start=(g == 0),
                             stop=(g == H_PASSES - 1),
                         )
                     if i + B_AHEAD < B_PIECES:
                         b_pieces.append(load_b_piece(i + B_AHEAD))
 
-                q_heads = finish.tile([P, ROUND_HEADS, D_HEAD], F32)
+                q_heads = finish.tile([P, heads, D_HEAD], F32, tag="q_heads_%d" % rnd)
                 q_flat = q_heads[:].rearrange("p h f -> p (h f)")
-                for bank in range(ROUND_BANKS):
-                    nc.scalar.copy(
-                        out=q_flat[:, BANK * bank : BANK * (bank + 1)], in_=q_banks[bank][:]
-                    )
+                for q_bank, (start, width) in zip(q_banks, slices):
+                    nc.scalar.copy(out=q_flat[:, start : start + width], in_=q_bank[:])
                 rope = q_heads[:, :, D_NOPE:D_HEAD]
                 pairs = rope.rearrange("p h (i two) -> p h i two", two=2)
-                neighbour = finish.tile([P, ROUND_HEADS, 2, D_ROPE // 2], F32, bufs=1)
+                neighbour = finish.tile([P, heads, 2, D_ROPE // 2], F32, tag="neighbour_%d" % rnd)
                 for two in range(2):
                     nc.vector.tensor_tensor(
                         out=neighbour[:, :, two, :],
                         in0=pairs[:, :, :, 1 - two],
                         in1=sin_planes[:, two, :]
                         .unsqueeze(1)
-                        .to_broadcast([P, ROUND_HEADS, D_ROPE // 2]),
+                        .to_broadcast([P, heads, D_ROPE // 2]),
                         op=ALU.mult,
                     )
                 nc.vector.tensor_tensor(
                     out=rope,
                     in0=rope,
-                    in1=cos_table.unsqueeze(1).to_broadcast([P, ROUND_HEADS, D_ROPE]),
+                    in1=cos_table.unsqueeze(1).to_broadcast([P, heads, D_ROPE]),
                     op=ALU.mult,
                 )
                 nc.vector.tensor_tensor(
@@ -359,7 +372,7 @@ def tile_multiheadlatentattention_pa_k_kernel(
                 store_queue = nc.sync if rnd == ROUNDS - 1 else nc.scalar
                 for b in range(BATCH):
                     store_queue.dma_start(
-                        out=out[b, ROUND_HEADS * rnd : ROUND_HEADS * (rnd + 1)].rearrange(
+                        out=out[b, first_head[rnd] : first_head[rnd] + heads].rearrange(
                             "h s f -> s h f"
                         ),
                         in_=q_heads[b:P:BATCH, :, :],

@@ -38,7 +38,7 @@ LAST_ROUND_HEADS = 4
 ROUND_HEADS = (HEADS - LAST_ROUND_HEADS, LAST_ROUND_HEADS)
 ROUNDS = len(ROUND_HEADS)
 B_PIECES = ROUNDS * H_PASSES
-B_AHEAD = 6
+B_AHEAD = 9
 
 ROUND_MAGIC = 12582912.0
 
@@ -60,59 +60,18 @@ def tile_multiheadlatentattention_pa_k_kernel(
     tc, x, Wqa_words, Wqa_scales, q_a_norm_w, Wqb_words, Wqb_scales, out
 ):
     nc = tc.nc
-    with ExitStack() as ctx:
-        keep = ctx.enter_context(tc.tile_pool(name="keep", bufs=1))
-        a_pool = ctx.enter_context(tc.tile_pool(name="a_pool", bufs=A_PIECES))
-        b_pool = ctx.enter_context(tc.tile_pool(name="b_pool", bufs=B_AHEAD))
-        stage = ctx.enter_context(tc.tile_pool(name="stage", bufs=4))
-        finish = ctx.enter_context(tc.tile_pool(name="finish", bufs=1))
+    first_head = [sum(ROUND_HEADS[:rnd]) for rnd in range(ROUNDS)]
 
+    with ExitStack() as whole_kernel:
+        keep = whole_kernel.enter_context(tc.tile_pool(name="keep", bufs=1))
+        b_pool = whole_kernel.enter_context(tc.tile_pool(name="b_pool", bufs=B_AHEAD))
 
-        a_planes = keep.tile([P, X_PASSES, A_QUARTER], U8, align_bytes=64)
+        c_gain = keep.tile([P, H_PASSES, P, PACK], F32)
+        rstd_all = keep.tile([P, P], F32)
+        table = keep.tile([P, 2 * D_ROPE], F32)
         b_planes = keep.tile([P, H_PASSES // PLANES, HEADS * D_HEAD], U8, align_bytes=64)
-        gain_rows = keep.tile([P, K_PASS], BF16)
-        nc.vector.memset(a_planes[:].rearrange("p g n -> p (g n)").bitcast(I32), 0)
-        nc.vector.memset(gain_rows[:], 0.0)
-        nc.vector.memset(b_planes[:].rearrange("p a n -> p (a n)").bitcast(I32), 0)
-
-        x_sb = keep.tile([P, D_MODEL], BF16)
-        for b in range(BATCH):
-            nc.sync.dma_start(out=x_sb[b:P:BATCH, :], in_=x[b])
-
-        nc.sync.dma_start(
-            out=gain_rows[0:H_PASSES, :],
-            in_=q_a_norm_w.rearrange("(g k) -> g k", g=H_PASSES),
-        )
-
-        for g in range(X_PASSES):
-            for quad in range(4):
-                nc.sync.dma_start(
-                    out=a_planes[32 * quad : 32 * quad + 16, g, :].bitcast(I32),
-                    in_=Wqa_scales[g, 4 * quad : 4 * quad + 4, :]
-                    .rearrange("r (j n) -> j r n", j=PLANES)
-                    .bitcast(I32),
-                )
-
-        a_words = Wqa_words.rearrange("g p n t -> p g (n t)")
-        a_pieces = []
-        for j in range(A_PIECES):
-            a_piece = a_pool.tile([P, X_PASSES, A_COLS], U32, align_bytes=64)
-            nc.sync.dma_start(
-                out=a_piece[:].bitcast(I32),
-                in_=a_words[:, :, PACK * A_COLS * j : PACK * A_COLS * (j + 1)].bitcast(I32),
-            )
-            a_pieces.append(a_piece)
-
-        for a in range(H_PASSES // PLANES):
-            for quad in range(4):
-                nc.sync.dma_start(
-                    out=b_planes[32 * quad : 32 * quad + 16, a, :].bitcast(I32),
-                    in_=Wqb_scales[
-                        PLANES * a : PLANES * (a + 1), 4 * quad : 4 * quad + 4, :
-                    ].bitcast(I32),
-                )
-
-        first_head = [sum(ROUND_HEADS[:rnd]) for rnd in range(ROUNDS)]
+        h_codes = keep.tile([P, H_PASSES, P], U32, align_bytes=64)
+        h_scales = keep.tile([P, H_PASSES, P], U8, align_bytes=64)
 
         def load_b_piece(i):
             rnd, g = divmod(i, H_PASSES)
@@ -127,80 +86,124 @@ def tile_multiheadlatentattention_pa_k_kernel(
             )
             return b_piece
 
-        b_pieces = [load_b_piece(i) for i in range(B_AHEAD)]
+        with ExitStack() as first_matmul:
+            once = first_matmul.enter_context(tc.tile_pool(name="once", bufs=1))
+            a_pool = first_matmul.enter_context(tc.tile_pool(name="a_pool", bufs=A_PIECES))
+            stage_c = first_matmul.enter_context(tc.tile_pool(name="stage_c", bufs=4))
+            psum_c = first_matmul.enter_context(tc.psum_pool(name="psum_c", bufs=4))
 
-        ident = keep.tile([P, P], F32)
-        masks.make_identity(nc, ident[:])
+            a_planes = once.tile([P, X_PASSES, A_QUARTER], U8, align_bytes=64)
+            gain_rows = once.tile([P, K_PASS], BF16)
+            nc.vector.memset(a_planes[:].rearrange("p g n -> p (g n)").bitcast(I32), 0)
+            nc.vector.memset(gain_rows[:], 0.0)
+            nc.vector.memset(b_planes[:].rearrange("p a n -> p (a n)").bitcast(I32), 0)
 
-        angle_index = keep.tile([P, 2 * D_ROPE], I32)
-        nc.gpsimd.iota(
-            angle_index[:, 0:D_ROPE], pattern=[[0, 2], [1, 64]], base=0, channel_multiplier=0
-        )
-        nc.gpsimd.iota(
-            angle_index[:, D_ROPE : 2 * D_ROPE],
-            pattern=[[1, 2], [0, 2], [2, 32]],
-            base=0,
-            channel_multiplier=0,
-        )
-        partition_index = keep.tile([P, 1], I32)
-        nc.gpsimd.iota(partition_index[:], pattern=[[0, 1]], base=0, channel_multiplier=1)
-        position_int = keep.tile([P, 1], I32)
-        nc.vector.tensor_single_scalar(
-            out=position_int[:], in_=partition_index[:], scalar=1, op=ALU.arith_shift_right
-        )
-        position = keep.tile([P, 1], F32)
-        nc.vector.tensor_copy(out=position[:], in_=position_int[:])
+            x_sb = once.tile([P, D_MODEL], BF16)
+            for b in range(BATCH):
+                nc.sync.dma_start(out=x_sb[b:P:BATCH, :], in_=x[b])
 
-        inv_freq = keep.tile([P, 2 * D_ROPE], F32)
-        nc.vector.tensor_copy(out=inv_freq[:], in_=angle_index[:])
-        nc.scalar.activation(
-            out=inv_freq[:], in_=inv_freq[:], func=ACT.Exp, scale=-math.log(THETA) / 64.0
-        )
-        angle = keep.tile([P, 2 * D_ROPE], F32)
-        nc.vector.tensor_scalar(
-            out=angle[:, 0:D_ROPE],
-            in0=inv_freq[:, 0:D_ROPE],
-            scalar1=position[:, 0:1],
-            scalar2=math.pi / 2.0,
-            op0=ALU.mult,
-            op1=ALU.add,
-        )
-        nc.vector.tensor_scalar_mul(
-            out=angle[:, D_ROPE : 2 * D_ROPE],
-            in0=inv_freq[:, D_ROPE : 2 * D_ROPE],
-            scalar1=position[:, 0:1],
-        )
-        whole_turns = keep.tile([P, 2 * D_ROPE], F32)
-        nc.vector.tensor_scalar(
-            out=whole_turns[:],
-            in0=angle[:],
-            scalar1=1.0 / (2.0 * math.pi),
-            scalar2=ROUND_MAGIC,
-            op0=ALU.mult,
-            op1=ALU.add,
-        )
-        nc.vector.tensor_scalar(
-            out=whole_turns[:],
-            in0=whole_turns[:],
-            scalar1=ROUND_MAGIC,
-            scalar2=2.0 * math.pi,
-            op0=ALU.subtract,
-            op1=ALU.mult,
-        )
-        nc.vector.tensor_sub(out=angle[:], in0=angle[:], in1=whole_turns[:])
-        table = keep.tile([P, 2 * D_ROPE], F32)
-        nc.scalar.activation(out=table[:], in_=angle[:], func=ACT.Sin)
-        cos_table = table[:, 0:D_ROPE]
-        sin_planes = table[:, D_ROPE : 2 * D_ROPE].rearrange("p (two i) -> p two i", two=2)
-        nc.vector.tensor_scalar_mul(
-            out=sin_planes[:, 0, :], in0=sin_planes[:, 0, :], scalar1=-1.0
-        )
+            nc.sync.dma_start(
+                out=gain_rows[0:H_PASSES, :],
+                in_=q_a_norm_w.rearrange("(g k) -> g k", g=H_PASSES),
+            )
 
-        square_sums = keep.tile([P, H_PASSES], F32)
-        c_gain = keep.tile([P, H_PASSES, P, PACK], F32)
-        rstd_all = keep.tile([P, P], F32)
+            for g in range(X_PASSES):
+                for quad in range(4):
+                    nc.sync.dma_start(
+                        out=a_planes[32 * quad : 32 * quad + 16, g, :].bitcast(I32),
+                        in_=Wqa_scales[g, 4 * quad : 4 * quad + 4, :]
+                        .rearrange("r (j n) -> j r n", j=PLANES)
+                        .bitcast(I32),
+                    )
 
-        with tc.psum_pool(name="psum_c", bufs=4) as psum_c:
+            a_words = Wqa_words.rearrange("g p n t -> p g (n t)")
+            a_pieces = []
+            for j in range(A_PIECES):
+                a_piece = a_pool.tile([P, X_PASSES, A_COLS], U32, align_bytes=64)
+                nc.sync.dma_start(
+                    out=a_piece[:].bitcast(I32),
+                    in_=a_words[:, :, PACK * A_COLS * j : PACK * A_COLS * (j + 1)].bitcast(I32),
+                )
+                a_pieces.append(a_piece)
+
+            b_pieces = [load_b_piece(i) for i in range(B_AHEAD)]
+
+            ident = once.tile([P, P], F32)
+            masks.make_identity(nc, ident[:])
+
+            angle_index = once.tile([P, 2 * D_ROPE], I32)
+            nc.gpsimd.iota(
+                angle_index[:, 0:D_ROPE], pattern=[[0, 2], [1, 64]], base=0, channel_multiplier=0
+            )
+            nc.gpsimd.iota(
+                angle_index[:, D_ROPE : 2 * D_ROPE],
+                pattern=[[1, 2], [0, 2], [2, 32]],
+                base=0,
+                channel_multiplier=0,
+            )
+            partition_index = once.tile([P, 1], I32)
+            nc.gpsimd.iota(partition_index[:], pattern=[[0, 1]], base=0, channel_multiplier=1)
+
+            for a in range(H_PASSES // PLANES):
+                for quad in range(4):
+                    nc.gpsimd.dma_start(
+                        out=b_planes[32 * quad : 32 * quad + 16, a, :].bitcast(F32),
+                        in_=Wqb_scales[
+                            PLANES * a : PLANES * (a + 1), 4 * quad : 4 * quad + 4, :
+                        ].bitcast(F32),
+                    )
+
+            position_int = once.tile([P, 1], I32)
+            nc.vector.tensor_single_scalar(
+                out=position_int[:], in_=partition_index[:], scalar=1, op=ALU.arith_shift_right
+            )
+            position = once.tile([P, 1], F32)
+            nc.vector.tensor_copy(out=position[:], in_=position_int[:])
+
+            inv_freq = once.tile([P, 2 * D_ROPE], F32)
+            nc.vector.tensor_copy(out=inv_freq[:], in_=angle_index[:])
+            nc.scalar.activation(
+                out=inv_freq[:], in_=inv_freq[:], func=ACT.Exp, scale=-math.log(THETA) / 64.0
+            )
+            angle = once.tile([P, 2 * D_ROPE], F32)
+            nc.vector.tensor_scalar(
+                out=angle[:, 0:D_ROPE],
+                in0=inv_freq[:, 0:D_ROPE],
+                scalar1=position[:, 0:1],
+                scalar2=math.pi / 2.0,
+                op0=ALU.mult,
+                op1=ALU.add,
+            )
+            nc.vector.tensor_scalar_mul(
+                out=angle[:, D_ROPE : 2 * D_ROPE],
+                in0=inv_freq[:, D_ROPE : 2 * D_ROPE],
+                scalar1=position[:, 0:1],
+            )
+            whole_turns = once.tile([P, 2 * D_ROPE], F32)
+            nc.vector.tensor_scalar(
+                out=whole_turns[:],
+                in0=angle[:],
+                scalar1=1.0 / (2.0 * math.pi),
+                scalar2=ROUND_MAGIC,
+                op0=ALU.mult,
+                op1=ALU.add,
+            )
+            nc.vector.tensor_scalar(
+                out=whole_turns[:],
+                in0=whole_turns[:],
+                scalar1=ROUND_MAGIC,
+                scalar2=2.0 * math.pi,
+                op0=ALU.subtract,
+                op1=ALU.mult,
+            )
+            nc.vector.tensor_sub(out=angle[:], in0=angle[:], in1=whole_turns[:])
+            nc.scalar.activation(out=table[:], in_=angle[:], func=ACT.Sin)
+            cos_table = table[:, 0:D_ROPE]
+            sin_planes = table[:, D_ROPE : 2 * D_ROPE].rearrange("p (two i) -> p two i", two=2)
+            nc.vector.tensor_scalar_mul(
+                out=sin_planes[:, 0, :], in0=sin_planes[:, 0, :], scalar1=-1.0
+            )
+
             x_words = x_sb[:].bitcast(F32)
             x_t = psum_c.tile([P, X_PASSES, 2, P], F32, tag="transposed")
             for g in range(X_PASSES):
@@ -210,28 +213,30 @@ def tile_multiheadlatentattention_pa_k_kernel(
                         x_words[:, 256 * g + u : 256 * (g + 1) : 2],
                         ident[:],
                     )
-            x_grouped = keep.tile([P, X_PASSES * P * PACK], BF16, align_bytes=64)
+            x_grouped = once.tile([P, X_PASSES * P * PACK], BF16, align_bytes=64)
             nc.vector.tensor_copy(
                 out=x_grouped[:].bitcast(F32).rearrange("p (g k u) -> p g k u", g=X_PASSES, u=2),
                 in_=x_t[:].rearrange("p g u k -> p g k u"),
             )
-            x_codes = keep.tile([P, X_PASSES * P], U32, align_bytes=64)
-            x_scales = keep.tile([P, X_PASSES * P], U8, align_bytes=64)
+            x_codes = once.tile([P, X_PASSES * P], U32, align_bytes=64)
+            x_scales = once.tile([P, X_PASSES * P], U8, align_bytes=64)
             nc.vector.quantize_mx(
                 out=x_codes[:].bitcast(FP8X4), scales=x_scales[:], in_=x_grouped[:]
             )
 
-            gain_sorted = keep.tile([P, PACK, P], F32)
+            gain_sorted = once.tile([P, PACK, P], F32)
             nc.vector.tensor_copy(
                 out=gain_sorted[:], in_=gain_rows[:].rearrange("g (p t) -> g t p", t=PACK)
             )
             gain_t = psum_c.tile([P, PACK, P], F32, tag="transposed")
             for t in range(PACK):
                 nc.tensor.transpose(gain_t[:, t, :], gain_sorted[:, t, :], ident[:])
-            gain = keep.tile([P, H_PASSES, PACK], F32)
+            gain = once.tile([P, H_PASSES, PACK], F32)
             nc.vector.tensor_copy(
                 out=gain[:], in_=gain_t[:, :, 0:H_PASSES].rearrange("p t g -> p g t")
             )
+
+            square_sums = once.tile([P, H_PASSES], F32)
 
             def multiply_piece(j):
                 sorted_banks = []
@@ -249,11 +254,11 @@ def tile_multiheadlatentattention_pa_k_kernel(
                             start=(xg == 0),
                             stop=(xg == X_PASSES - 1),
                         )
-                    c_sorted = stage.tile([P, PACK, P], F32)
+                    c_sorted = stage_c.tile([P, PACK, P], F32)
                     nc.scalar.copy(
                         out=c_sorted[:], in_=c_bank[:].rearrange("k (p t) -> k t p", t=PACK)
                     )
-                    squares = stage.tile([P, BANK], BF16, bufs=2)
+                    squares = stage_c.tile([P, BANK], BF16, bufs=2)
                     nc.scalar.activation(
                         out=squares[:],
                         in_=c_bank[:],
@@ -282,7 +287,7 @@ def tile_multiheadlatentattention_pa_k_kernel(
                 waiting = arrived
             transpose_piece(waiting)
 
-            mean_square = keep.tile([P, 1], F32)
+            mean_square = once.tile([P, 1], F32)
             nc.vector.reduce_sum(out=mean_square[:], in_=square_sums[:], axis=AXIS.X)
             nc.vector.tensor_scalar(
                 out=mean_square[:],
@@ -292,30 +297,32 @@ def tile_multiheadlatentattention_pa_k_kernel(
                 op0=ALU.mult,
                 op1=ALU.add,
             )
-            rstd = keep.tile([P, 1], F32)
+            rstd = once.tile([P, 1], F32)
             nc.scalar.sqrt(out=rstd[:], in_=mean_square[:])
             nc.vector.reciprocal(out=rstd[:], in_=rstd[:])
             rstd_t = psum_c.tile([P, P], F32, tag="transposed")
             nc.tensor.transpose(rstd_t[:], rstd[:, 0:1].to_broadcast([P, P]), ident[:])
             nc.vector.tensor_copy(out=rstd_all[:], in_=rstd_t[:])
 
-        h_codes = keep.tile([P, H_PASSES, P], U32, align_bytes=64)
-        h_scales = keep.tile([P, H_PASSES, P], U8, align_bytes=64)
-        for g in range(H_PASSES):
-            h_grouped = stage.tile([P, P, PACK], BF16, align_bytes=64)
-            nc.vector.tensor_tensor(
-                out=h_grouped[:],
-                in0=c_gain[:, g, :, :],
-                in1=rstd_all[:].unsqueeze(2).to_broadcast([P, P, PACK]),
-                op=ALU.mult,
-            )
-            nc.vector.quantize_mx(
-                out=h_codes[:, g, :].bitcast(FP8X4),
-                scales=h_scales[:, g, :],
-                in_=h_grouped[:].rearrange("p k t -> p (k t)"),
-            )
+        with ExitStack() as second_matmul:
+            stage_h = second_matmul.enter_context(tc.tile_pool(name="stage_h", bufs=4))
+            finish = second_matmul.enter_context(tc.tile_pool(name="finish", bufs=1))
+            psum_q = second_matmul.enter_context(tc.psum_pool(name="psum_q", bufs=1))
 
-        with tc.psum_pool(name="psum_q", bufs=1) as psum_q:
+            for g in range(H_PASSES):
+                h_grouped = stage_h.tile([P, P, PACK], BF16, align_bytes=64)
+                nc.vector.tensor_tensor(
+                    out=h_grouped[:],
+                    in0=c_gain[:, g, :, :],
+                    in1=rstd_all[:].unsqueeze(2).to_broadcast([P, P, PACK]),
+                    op=ALU.mult,
+                )
+                nc.vector.quantize_mx(
+                    out=h_codes[:, g, :].bitcast(FP8X4),
+                    scales=h_scales[:, g, :],
+                    in_=h_grouped[:].rearrange("p k t -> p (k t)"),
+                )
+
             for rnd in range(ROUNDS):
                 heads = ROUND_HEADS[rnd]
                 first_col = first_head[rnd] * D_HEAD

@@ -29,8 +29,10 @@ EPS = 1e-6
 X_PASSES = D_MODEL // K_PASS
 H_PASSES = RANK // K_PASS
 
-A_COLS = 2 * BANK
+A_COLS = 4 * BANK
 A_PIECES = RANK // A_COLS
+STEP_BANKS = 2
+STEPS = RANK // (STEP_BANKS * BANK)
 PLANES = 4
 A_QUARTER = RANK // PLANES
 
@@ -107,15 +109,6 @@ def tile_multiheadlatentattention_pa_k_kernel(
                 in_=q_a_norm_w.rearrange("(g k) -> g k", g=H_PASSES),
             )
 
-            for g in range(X_PASSES):
-                for quad in range(4):
-                    nc.sync.dma_start(
-                        out=a_planes[32 * quad : 32 * quad + 16, g, :].bitcast(I32),
-                        in_=Wqa_scales[g, 4 * quad : 4 * quad + 4, :]
-                        .rearrange("r (j n) -> j r n", j=PLANES)
-                        .bitcast(I32),
-                    )
-
             a_words = Wqa_words.rearrange("g p n t -> p g (n t)")
             a_pieces = []
             for j in range(A_PIECES):
@@ -144,6 +137,14 @@ def tile_multiheadlatentattention_pa_k_kernel(
             partition_index = once.tile([P, 1], I32)
             nc.gpsimd.iota(partition_index[:], pattern=[[0, 1]], base=0, channel_multiplier=1)
 
+            for g in range(X_PASSES):
+                for quad in range(4):
+                    nc.gpsimd.dma_start(
+                        out=a_planes[32 * quad : 32 * quad + 16, g, :].bitcast(F32),
+                        in_=Wqa_scales[g, 4 * quad : 4 * quad + 4, :]
+                        .rearrange("r (j n) -> j r n", j=PLANES)
+                        .bitcast(F32),
+                    )
             for a in range(H_PASSES // PLANES):
                 for quad in range(4):
                     nc.gpsimd.dma_start(
@@ -238,10 +239,10 @@ def tile_multiheadlatentattention_pa_k_kernel(
 
             square_sums = once.tile([P, H_PASSES], F32)
 
-            def multiply_piece(j):
+            def multiply_step(step):
                 sorted_banks = []
-                for half in range(A_COLS // BANK):
-                    g = (A_COLS // BANK) * j + half
+                for g in range(STEP_BANKS * step, STEP_BANKS * (step + 1)):
+                    j, piece_col = divmod(BANK * g, A_COLS)
                     plane, plane_col = divmod(BANK * g, A_QUARTER)
                     c_bank = psum_c.tile([P, BANK], F32, tag="c_bank")
                     for xg in range(X_PASSES):
@@ -249,15 +250,17 @@ def tile_multiheadlatentattention_pa_k_kernel(
                             out=c_bank[:],
                             lhsT=x_codes[:, P * xg : P * (xg + 1)].bitcast(FP8X4),
                             lhsT_scale=x_scales[:, P * xg : P * (xg + 1)],
-                            rhs=a_pieces[j][:, xg, BANK * half : BANK * (half + 1)].bitcast(FP8X4),
+                            rhs=a_pieces[j][:, xg, piece_col : piece_col + BANK].bitcast(FP8X4),
                             rhs_scale=a_planes[4 * plane : P, xg, plane_col : plane_col + BANK],
                             start=(xg == 0),
                             stop=(xg == X_PASSES - 1),
                         )
                     c_sorted = stage_c.tile([P, PACK, P], F32)
-                    nc.scalar.copy(
-                        out=c_sorted[:], in_=c_bank[:].rearrange("k (p t) -> k t p", t=PACK)
-                    )
+                    by_t = c_bank[:].rearrange("k (p t) -> k t p", t=PACK)
+                    if g % 2 == 0:
+                        nc.scalar.copy(out=c_sorted[:], in_=by_t)
+                    else:
+                        nc.vector.tensor_copy(out=c_sorted[:], in_=by_t)
                     squares = stage_c.tile([P, BANK], BF16, bufs=2)
                     nc.scalar.activation(
                         out=squares[:],
@@ -268,7 +271,7 @@ def tile_multiheadlatentattention_pa_k_kernel(
                     sorted_banks.append((g, c_sorted))
                 return sorted_banks
 
-            def transpose_piece(sorted_banks):
+            def transpose_step(sorted_banks):
                 for g, c_sorted in sorted_banks:
                     c_t = psum_c.tile([P, PACK, P], F32, tag="transposed")
                     for t in range(PACK):
@@ -280,12 +283,12 @@ def tile_multiheadlatentattention_pa_k_kernel(
                         op=ALU.mult,
                     )
 
-            waiting = multiply_piece(0)
-            for j in range(1, A_PIECES):
-                arrived = multiply_piece(j)
-                transpose_piece(waiting)
+            waiting = multiply_step(0)
+            for step in range(1, STEPS):
+                arrived = multiply_step(step)
+                transpose_step(waiting)
                 waiting = arrived
-            transpose_piece(waiting)
+            transpose_step(waiting)
 
             mean_square = once.tile([P, 1], F32)
             nc.vector.reduce_sum(out=mean_square[:], in_=square_sums[:], axis=AXIS.X)

@@ -29,10 +29,8 @@ EPS = 1e-6
 X_PASSES = D_MODEL // K_PASS
 H_PASSES = RANK // K_PASS
 
-A_COLS = 4 * BANK
+A_COLS = 2 * BANK
 A_PIECES = RANK // A_COLS
-STEP_BANKS = 2
-STEPS = RANK // (STEP_BANKS * BANK)
 PLANES = 4
 A_QUARTER = RANK // PLANES
 
@@ -109,6 +107,15 @@ def tile_multiheadlatentattention_pa_k_kernel(
                 in_=q_a_norm_w.rearrange("(g k) -> g k", g=H_PASSES),
             )
 
+            for g in range(X_PASSES):
+                for quad in range(4):
+                    nc.sync.dma_start(
+                        out=a_planes[32 * quad : 32 * quad + 16, g, :].bitcast(I32),
+                        in_=Wqa_scales[g, 4 * quad : 4 * quad + 4, :]
+                        .rearrange("r (j n) -> j r n", j=PLANES)
+                        .bitcast(I32),
+                    )
+
             a_words = Wqa_words.rearrange("g p n t -> p g (n t)")
             a_pieces = []
             for j in range(A_PIECES):
@@ -137,14 +144,6 @@ def tile_multiheadlatentattention_pa_k_kernel(
             partition_index = once.tile([P, 1], I32)
             nc.gpsimd.iota(partition_index[:], pattern=[[0, 1]], base=0, channel_multiplier=1)
 
-            for g in range(X_PASSES):
-                for quad in range(4):
-                    nc.gpsimd.dma_start(
-                        out=a_planes[32 * quad : 32 * quad + 16, g, :].bitcast(F32),
-                        in_=Wqa_scales[g, 4 * quad : 4 * quad + 4, :]
-                        .rearrange("r (j n) -> j r n", j=PLANES)
-                        .bitcast(F32),
-                    )
             for a in range(H_PASSES // PLANES):
                 for quad in range(4):
                     nc.gpsimd.dma_start(
@@ -239,10 +238,10 @@ def tile_multiheadlatentattention_pa_k_kernel(
 
             square_sums = once.tile([P, H_PASSES], F32)
 
-            def multiply_step(step):
+            def multiply_piece(j):
                 sorted_banks = []
-                for g in range(STEP_BANKS * step, STEP_BANKS * (step + 1)):
-                    j, piece_col = divmod(BANK * g, A_COLS)
+                for half in range(A_COLS // BANK):
+                    g = (A_COLS // BANK) * j + half
                     plane, plane_col = divmod(BANK * g, A_QUARTER)
                     c_bank = psum_c.tile([P, BANK], F32, tag="c_bank")
                     for xg in range(X_PASSES):
@@ -250,17 +249,15 @@ def tile_multiheadlatentattention_pa_k_kernel(
                             out=c_bank[:],
                             lhsT=x_codes[:, P * xg : P * (xg + 1)].bitcast(FP8X4),
                             lhsT_scale=x_scales[:, P * xg : P * (xg + 1)],
-                            rhs=a_pieces[j][:, xg, piece_col : piece_col + BANK].bitcast(FP8X4),
+                            rhs=a_pieces[j][:, xg, BANK * half : BANK * (half + 1)].bitcast(FP8X4),
                             rhs_scale=a_planes[4 * plane : P, xg, plane_col : plane_col + BANK],
                             start=(xg == 0),
                             stop=(xg == X_PASSES - 1),
                         )
                     c_sorted = stage_c.tile([P, PACK, P], F32)
-                    by_t = c_bank[:].rearrange("k (p t) -> k t p", t=PACK)
-                    if g % 2 == 0:
-                        nc.scalar.copy(out=c_sorted[:], in_=by_t)
-                    else:
-                        nc.vector.tensor_copy(out=c_sorted[:], in_=by_t)
+                    nc.scalar.copy(
+                        out=c_sorted[:], in_=c_bank[:].rearrange("k (p t) -> k t p", t=PACK)
+                    )
                     squares = stage_c.tile([P, BANK], BF16, bufs=2)
                     nc.scalar.activation(
                         out=squares[:],
@@ -271,7 +268,7 @@ def tile_multiheadlatentattention_pa_k_kernel(
                     sorted_banks.append((g, c_sorted))
                 return sorted_banks
 
-            def transpose_step(sorted_banks):
+            def transpose_piece(sorted_banks):
                 for g, c_sorted in sorted_banks:
                     c_t = psum_c.tile([P, PACK, P], F32, tag="transposed")
                     for t in range(PACK):
@@ -283,12 +280,12 @@ def tile_multiheadlatentattention_pa_k_kernel(
                         op=ALU.mult,
                     )
 
-            waiting = multiply_step(0)
-            for step in range(1, STEPS):
-                arrived = multiply_step(step)
-                transpose_step(waiting)
+            waiting = multiply_piece(0)
+            for j in range(1, A_PIECES):
+                arrived = multiply_piece(j)
+                transpose_piece(waiting)
                 waiting = arrived
-            transpose_step(waiting)
+            transpose_piece(waiting)
 
             mean_square = once.tile([P, 1], F32)
             nc.vector.reduce_sum(out=mean_square[:], in_=square_sums[:], axis=AXIS.X)
@@ -326,6 +323,7 @@ def tile_multiheadlatentattention_pa_k_kernel(
                     in_=h_grouped[:].rearrange("p k t -> p (k t)"),
                 )
 
+            rotated = []
             for rnd in range(ROUNDS):
                 heads = ROUND_HEADS[rnd]
                 first_col = first_head[rnd] * D_HEAD
@@ -353,8 +351,13 @@ def tile_multiheadlatentattention_pa_k_kernel(
 
                 q_heads = finish.tile([P, heads, D_HEAD], F32, tag="q_heads_%d" % rnd)
                 q_flat = q_heads[:].rearrange("p h f -> p (h f)")
-                for q_bank, (start, width) in zip(q_banks, slices):
-                    nc.scalar.copy(out=q_flat[:, start : start + width], in_=q_bank[:])
+                for n, (start, width) in enumerate(slices):
+                    if n % 2 == 0:
+                        nc.scalar.copy(out=q_flat[:, start : start + width], in_=q_banks[n][:])
+                    else:
+                        nc.vector.tensor_copy(
+                            out=q_flat[:, start : start + width], in_=q_banks[n][:]
+                        )
                 rope = q_heads[:, :, D_NOPE:D_HEAD]
                 pairs = rope.rearrange("p h (i two) -> p h i two", two=2)
                 neighbour = finish.tile([P, heads, 2, D_ROPE // 2], F32, tag="neighbour_%d" % rnd)
@@ -379,11 +382,13 @@ def tile_multiheadlatentattention_pa_k_kernel(
                     in1=neighbour[:].rearrange("p h two i -> p h i two"),
                     op=ALU.add,
                 )
-                store_queue = nc.sync if rnd == ROUNDS - 1 else nc.scalar
+                rotated.append(q_heads)
+
+            for rnd in range(ROUNDS):
                 for b in range(BATCH):
-                    store_queue.dma_start(
-                        out=out[b, first_head[rnd] : first_head[rnd] + heads].rearrange(
+                    nc.sync.dma_start(
+                        out=out[b, first_head[rnd] : first_head[rnd] + ROUND_HEADS[rnd]].rearrange(
                             "h s f -> s h f"
                         ),
-                        in_=q_heads[b:P:BATCH, :, :],
+                        in_=rotated[rnd][b:P:BATCH, :, :],
                     )

@@ -38,7 +38,8 @@ LAST_ROUND_HEADS = 4
 ROUND_HEADS = (HEADS - LAST_ROUND_HEADS, LAST_ROUND_HEADS)
 ROUNDS = len(ROUND_HEADS)
 B_PIECES = ROUNDS * H_PASSES
-B_AHEAD = 9
+RING = 16
+B_AHEAD = RING - A_PIECES
 
 ROUND_MAGIC = 12582912.0
 
@@ -64,7 +65,7 @@ def tile_multiheadlatentattention_pa_k_kernel(
 
     with ExitStack() as whole_kernel:
         keep = whole_kernel.enter_context(tc.tile_pool(name="keep", bufs=1))
-        b_pool = whole_kernel.enter_context(tc.tile_pool(name="b_pool", bufs=B_AHEAD))
+        ring = whole_kernel.enter_context(tc.tile_pool(name="ring", bufs=RING))
 
         c_gain = keep.tile([P, H_PASSES, P, PACK], F32)
         rstd_all = keep.tile([P, P], F32)
@@ -77,7 +78,7 @@ def tile_multiheadlatentattention_pa_k_kernel(
             rnd, g = divmod(i, H_PASSES)
             first_col = first_head[rnd] * D_HEAD
             cols = ROUND_HEADS[rnd] * D_HEAD
-            b_piece = b_pool.tile([P, cols], U32, align_bytes=64)
+            b_piece = ring.tile([P, cols], U32, align_bytes=64, tag="piece")
             nc.sync.dma_start(
                 out=b_piece[:].bitcast(I32),
                 in_=Wqb_words[g]
@@ -88,7 +89,6 @@ def tile_multiheadlatentattention_pa_k_kernel(
 
         with ExitStack() as first_matmul:
             once = first_matmul.enter_context(tc.tile_pool(name="once", bufs=1))
-            a_pool = first_matmul.enter_context(tc.tile_pool(name="a_pool", bufs=A_PIECES))
             stage_c = first_matmul.enter_context(tc.tile_pool(name="stage_c", bufs=4))
             psum_c = first_matmul.enter_context(tc.psum_pool(name="psum_c", bufs=4))
 
@@ -100,26 +100,17 @@ def tile_multiheadlatentattention_pa_k_kernel(
 
             x_sb = once.tile([P, D_MODEL], BF16)
             for b in range(BATCH):
-                nc.sync.dma_start(out=x_sb[b:P:BATCH, :], in_=x[b])
+                nc.scalar.dma_start(out=x_sb[b:P:BATCH, :], in_=x[b])
 
-            nc.sync.dma_start(
+            nc.scalar.dma_start(
                 out=gain_rows[0:H_PASSES, :],
                 in_=q_a_norm_w.rearrange("(g k) -> g k", g=H_PASSES),
             )
 
-            for g in range(X_PASSES):
-                for quad in range(4):
-                    nc.sync.dma_start(
-                        out=a_planes[32 * quad : 32 * quad + 16, g, :].bitcast(I32),
-                        in_=Wqa_scales[g, 4 * quad : 4 * quad + 4, :]
-                        .rearrange("r (j n) -> j r n", j=PLANES)
-                        .bitcast(I32),
-                    )
-
             a_words = Wqa_words.rearrange("g p n t -> p g (n t)")
             a_pieces = []
             for j in range(A_PIECES):
-                a_piece = a_pool.tile([P, X_PASSES, A_COLS], U32, align_bytes=64)
+                a_piece = ring.tile([P, X_PASSES, A_COLS], U32, align_bytes=64, tag="piece")
                 nc.sync.dma_start(
                     out=a_piece[:].bitcast(I32),
                     in_=a_words[:, :, PACK * A_COLS * j : PACK * A_COLS * (j + 1)].bitcast(I32),
@@ -130,6 +121,15 @@ def tile_multiheadlatentattention_pa_k_kernel(
 
             ident = once.tile([P, P], F32)
             masks.make_identity(nc, ident[:])
+
+            for g in range(X_PASSES):
+                for quad in range(4):
+                    nc.gpsimd.dma_start(
+                        out=a_planes[32 * quad : 32 * quad + 16, g, :].bitcast(F32),
+                        in_=Wqa_scales[g, 4 * quad : 4 * quad + 4, :]
+                        .rearrange("r (j n) -> j r n", j=PLANES)
+                        .bitcast(F32),
+                    )
 
             angle_index = once.tile([P, 2 * D_ROPE], I32)
             nc.gpsimd.iota(
@@ -281,8 +281,10 @@ def tile_multiheadlatentattention_pa_k_kernel(
                     )
 
             waiting = multiply_piece(0)
+            b_pieces.append(load_b_piece(B_AHEAD))
             for j in range(1, A_PIECES):
                 arrived = multiply_piece(j)
+                b_pieces.append(load_b_piece(B_AHEAD + j))
                 transpose_piece(waiting)
                 waiting = arrived
             transpose_piece(waiting)
@@ -346,8 +348,8 @@ def tile_multiheadlatentattention_pa_k_kernel(
                             start=(g == 0),
                             stop=(g == H_PASSES - 1),
                         )
-                    if i + B_AHEAD < B_PIECES:
-                        b_pieces.append(load_b_piece(i + B_AHEAD))
+                    if i + RING < B_PIECES:
+                        b_pieces.append(load_b_piece(i + RING))
 
                 q_heads = finish.tile([P, heads, D_HEAD], F32, tag="q_heads_%d" % rnd)
                 q_flat = q_heads[:].rearrange("p h f -> p (h f)")

@@ -34,11 +34,11 @@ A_PIECES = RANK // A_COLS
 PLANES = 4
 A_QUARTER = RANK // PLANES
 
-LAST_ROUND_HEADS = 4
-ROUND_HEADS = (HEADS - LAST_ROUND_HEADS, LAST_ROUND_HEADS)
-ROUNDS = len(ROUND_HEADS)
-B_PIECES = ROUNDS * H_PASSES
-RING = 16
+GROUP_HEADS = (8, 6, 2)
+GROUPS = len(GROUP_HEADS)
+WHOLE_ROW_PASSES = 6
+TWO_GROUP_PASSES = 6
+RING = 12
 B_AHEAD = RING - A_PIECES
 
 ROUND_MAGIC = 12582912.0
@@ -57,11 +57,22 @@ def moving_slices(cols):
     return slices
 
 
+def piece_plan():
+    split_from = WHOLE_ROW_PASSES + TWO_GROUP_PASSES
+    plan = [(g, 0, GROUPS) for g in range(WHOLE_ROW_PASSES)]
+    plan += [(g, 0, 2) for g in range(WHOLE_ROW_PASSES, split_from)]
+    plan += [(g, 0, 1) for g in range(split_from, H_PASSES)]
+    plan += [(g, 1, 1) for g in range(split_from, H_PASSES)]
+    plan += [(g, 2, 1) for g in range(WHOLE_ROW_PASSES, H_PASSES)]
+    return plan
+
+
 def tile_multiheadlatentattention_pa_k_kernel(
     tc, x, Wqa_words, Wqa_scales, q_a_norm_w, Wqb_words, Wqb_scales, out
 ):
     nc = tc.nc
-    first_head = [sum(ROUND_HEADS[:rnd]) for rnd in range(ROUNDS)]
+    first_head = [sum(GROUP_HEADS[:grp]) for grp in range(GROUPS)]
+    plan = piece_plan()
 
     with ExitStack() as whole_kernel:
         keep = whole_kernel.enter_context(tc.tile_pool(name="keep", bufs=1))
@@ -70,14 +81,15 @@ def tile_multiheadlatentattention_pa_k_kernel(
         c_gain = keep.tile([P, H_PASSES, P, PACK], F32)
         rstd_all = keep.tile([P, P], F32)
         table = keep.tile([P, 2 * D_ROPE], F32)
+        cos_wide = keep.tile([P, D_NOPE + D_HEAD], F32)
         b_planes = keep.tile([P, H_PASSES // PLANES, HEADS * D_HEAD], U8, align_bytes=64)
         h_codes = keep.tile([P, H_PASSES, P], U32, align_bytes=64)
         h_scales = keep.tile([P, H_PASSES, P], U8, align_bytes=64)
 
         def load_b_piece(i):
-            rnd, g = divmod(i, H_PASSES)
-            first_col = first_head[rnd] * D_HEAD
-            cols = ROUND_HEADS[rnd] * D_HEAD
+            g, first_group, groups = plan[i]
+            first_col = first_head[first_group] * D_HEAD
+            cols = sum(GROUP_HEADS[first_group : first_group + groups]) * D_HEAD
             b_piece = ring.tile([P, cols], U32, align_bytes=64, tag="piece")
             nc.sync.dma_start(
                 out=b_piece[:].bitcast(I32),
@@ -96,6 +108,7 @@ def tile_multiheadlatentattention_pa_k_kernel(
             gain_rows = once.tile([P, K_PASS], BF16)
             nc.vector.memset(a_planes[:].rearrange("p g n -> p (g n)").bitcast(I32), 0)
             nc.vector.memset(gain_rows[:], 0.0)
+            nc.vector.memset(cos_wide[:], 1.0)
             nc.vector.memset(b_planes[:].rearrange("p a n -> p (a n)").bitcast(I32), 0)
 
             x_sb = once.tile([P, D_MODEL], BF16)
@@ -199,6 +212,7 @@ def tile_multiheadlatentattention_pa_k_kernel(
             nc.vector.tensor_sub(out=angle[:], in0=angle[:], in1=whole_turns[:])
             nc.scalar.activation(out=table[:], in_=angle[:], func=ACT.Sin)
             cos_table = table[:, 0:D_ROPE]
+            nc.vector.tensor_copy(out=cos_wide[:, D_NOPE:D_HEAD], in_=cos_table)
             sin_planes = table[:, D_ROPE : 2 * D_ROPE].rearrange("p (two i) -> p two i", two=2)
             nc.vector.tensor_scalar_mul(
                 out=sin_planes[:, 0, :], in0=sin_planes[:, 0, :], scalar1=-1.0
@@ -325,44 +339,39 @@ def tile_multiheadlatentattention_pa_k_kernel(
                     in_=h_grouped[:].rearrange("p k t -> p (k t)"),
                 )
 
-            rotated = []
-            for rnd in range(ROUNDS):
-                heads = ROUND_HEADS[rnd]
-                first_col = first_head[rnd] * D_HEAD
-                slices = moving_slices(heads * D_HEAD)
-                q_banks = []
-                for n, (start, width) in enumerate(slices):
-                    q_bank = psum_q.tile([P, width], F32, tag="q_bank_%d_%d" % (rnd, n))
-                    q_banks.append(q_bank)
-                for g in range(H_PASSES):
-                    i = H_PASSES * rnd + g
-                    a, plane = divmod(g, PLANES)
-                    for q_bank, (start, width) in zip(q_banks, slices):
-                        col = first_col + start
-                        nc.tensor.matmul_mx(
-                            out=q_bank[:],
-                            lhsT=h_codes[:, g, :].bitcast(FP8X4),
-                            lhsT_scale=h_scales[:, g, :],
-                            rhs=b_pieces[i][:, start : start + width].bitcast(FP8X4),
-                            rhs_scale=b_planes[4 * plane : P, a, col : col + width],
-                            start=(g == 0),
-                            stop=(g == H_PASSES - 1),
-                        )
-                    if i + RING < B_PIECES:
-                        b_pieces.append(load_b_piece(i + RING))
+            slices = [moving_slices(heads * D_HEAD) for heads in GROUP_HEADS]
+            q_banks = []
+            for grp in range(GROUPS):
+                group_banks = []
+                for n, (start, width) in enumerate(slices[grp]):
+                    q_bank = psum_q.tile([P, width], F32, tag="q_bank_%d_%d" % (grp, n))
+                    group_banks.append(q_bank)
+                q_banks.append(group_banks)
 
-                q_heads = finish.tile([P, heads, D_HEAD], F32, tag="q_heads_%d" % rnd)
+            def add_neighbours(q_heads, turned, neighbour):
+                nc.vector.tensor_tensor(
+                    out=q_heads[:, :, D_NOPE:D_HEAD].rearrange("p h (i two) -> p h i two", two=2),
+                    in0=turned.rearrange("p h (i two) -> p h i two", two=2),
+                    in1=neighbour[:].rearrange("p h two i -> p h i two"),
+                    op=ALU.add,
+                )
+
+            def rotate_group(grp):
+                heads = GROUP_HEADS[grp]
+                q_heads = finish.tile([P, heads, D_HEAD], F32, tag="q_heads_%d" % grp)
                 q_flat = q_heads[:].rearrange("p h f -> p (h f)")
-                for n, (start, width) in enumerate(slices):
-                    if n % 2 == 0:
-                        nc.scalar.copy(out=q_flat[:, start : start + width], in_=q_banks[n][:])
-                    else:
-                        nc.vector.tensor_copy(
-                            out=q_flat[:, start : start + width], in_=q_banks[n][:]
-                        )
+                for n, (start, width) in enumerate(slices[grp]):
+                    nc.scalar.copy(out=q_flat[:, start : start + width], in_=q_banks[grp][n][:])
                 rope = q_heads[:, :, D_NOPE:D_HEAD]
                 pairs = rope.rearrange("p h (i two) -> p h i two", two=2)
-                neighbour = finish.tile([P, heads, 2, D_ROPE // 2], F32, tag="neighbour_%d" % rnd)
+                neighbour = finish.tile([P, heads, 2, D_ROPE // 2], F32, tag="neighbour_%d" % grp)
+                turned = finish.tile([P, heads, D_ROPE], F32, tag="turned_%d" % grp)
+                nc.vector.tensor_tensor(
+                    out=turned[:],
+                    in0=rope,
+                    in1=cos_table.unsqueeze(1).to_broadcast([P, heads, D_ROPE]),
+                    op=ALU.mult,
+                )
                 for two in range(2):
                     nc.vector.tensor_tensor(
                         out=neighbour[:, :, two, :],
@@ -372,25 +381,70 @@ def tile_multiheadlatentattention_pa_k_kernel(
                         .to_broadcast([P, heads, D_ROPE // 2]),
                         op=ALU.mult,
                     )
-                nc.vector.tensor_tensor(
-                    out=rope,
-                    in0=rope,
-                    in1=cos_table.unsqueeze(1).to_broadcast([P, heads, D_ROPE]),
-                    op=ALU.mult,
-                )
-                nc.vector.tensor_tensor(
-                    out=pairs,
-                    in0=pairs,
-                    in1=neighbour[:].rearrange("p h two i -> p h i two"),
-                    op=ALU.add,
-                )
-                rotated.append(q_heads)
+                add_neighbours(q_heads, turned[:], neighbour)
+                return q_heads
 
-            for rnd in range(ROUNDS):
+            def rotate_last_group(grp):
+                q_heads = finish.tile([P, 2, D_HEAD], F32, tag="q_heads_%d" % grp)
+                q_flat = q_heads[:].rearrange("p h f -> p (h f)")
+                neighbour = finish.tile([P, 2, 2, D_ROPE // 2], F32, tag="neighbour_%d" % grp)
+                wide_bank, rope_bank = q_banks[grp]
+                nc.vector.tensor_tensor(
+                    out=q_flat[:, 0 : D_NOPE + D_HEAD], in0=wide_bank[:], in1=cos_wide[:], op=ALU.mult
+                )
+                bank_ropes = (wide_bank[:, D_NOPE:D_HEAD], rope_bank[:])
+                for head in range(2):
+                    if head == 1:
+                        nc.vector.tensor_tensor(
+                            out=q_heads[:, 1, D_NOPE:D_HEAD],
+                            in0=rope_bank[:],
+                            in1=cos_table,
+                            op=ALU.mult,
+                        )
+                    bank_pairs = bank_ropes[head].rearrange("p (i two) -> p i two", two=2)
+                    for two in range(2):
+                        nc.vector.tensor_tensor(
+                            out=neighbour[:, head, two, :],
+                            in0=bank_pairs[:, :, 1 - two],
+                            in1=sin_planes[:, two, :],
+                            op=ALU.mult,
+                        )
+                add_neighbours(q_heads, q_heads[:, :, D_NOPE:D_HEAD], neighbour)
+                return q_heads
+
+            rotated = []
+            for i, (g, first_group, groups) in enumerate(plan):
+                a, plane = divmod(g, PLANES)
+                for grp in range(first_group, first_group + groups):
+                    group_col = first_head[grp] * D_HEAD
+                    piece_col = group_col - first_head[first_group] * D_HEAD
+                    for q_bank, (start, width) in zip(q_banks[grp], slices[grp]):
+                        nc.tensor.matmul_mx(
+                            out=q_bank[:],
+                            lhsT=h_codes[:, g, :].bitcast(FP8X4),
+                            lhsT_scale=h_scales[:, g, :],
+                            rhs=b_pieces[i][
+                                :, piece_col + start : piece_col + start + width
+                            ].bitcast(FP8X4),
+                            rhs_scale=b_planes[
+                                4 * plane : P, a, group_col + start : group_col + start + width
+                            ],
+                            start=(g == 0),
+                            stop=(g == H_PASSES - 1),
+                        )
+                if i + RING < len(plan):
+                    b_pieces.append(load_b_piece(i + RING))
+                if g == H_PASSES - 1:
+                    if first_group == GROUPS - 1:
+                        rotated.append(rotate_last_group(first_group))
+                    else:
+                        rotated.append(rotate_group(first_group))
+
+            for grp in range(GROUPS):
                 for b in range(BATCH):
                     nc.sync.dma_start(
-                        out=out[b, first_head[rnd] : first_head[rnd] + ROUND_HEADS[rnd]].rearrange(
+                        out=out[b, first_head[grp] : first_head[grp] + GROUP_HEADS[grp]].rearrange(
                             "h s f -> s h f"
                         ),
-                        in_=rotated[rnd][b:P:BATCH, :, :],
+                        in_=rotated[grp][b:P:BATCH, :, :],
                     )

@@ -29,8 +29,10 @@ EPS = 1e-6
 X_PASSES = D_MODEL // K_PASS
 H_PASSES = RANK // K_PASS
 
-A_COLS = 2 * BANK
-A_PIECES = RANK // A_COLS
+A_BLOCK_COLS = (3072, 3072, 2048)
+A_PIECES = X_PASSES * len(A_BLOCK_COLS)
+STEP_BANKS = 2
+STEPS = RANK // (STEP_BANKS * BANK)
 PLANES = 4
 A_QUARTER = RANK // PLANES
 
@@ -120,15 +122,20 @@ def tile_multiheadlatentattention_pa_k_kernel(
                 in_=q_a_norm_w.rearrange("(g k) -> g k", g=H_PASSES),
             )
 
-            a_words = Wqa_words.rearrange("g p n t -> p g (n t)")
-            a_pieces = []
-            for j in range(A_PIECES):
-                a_piece = ring.tile([P, X_PASSES, A_COLS], U32, align_bytes=64, tag="piece")
-                nc.sync.dma_start(
-                    out=a_piece[:].bitcast(I32),
-                    in_=a_words[:, :, PACK * A_COLS * j : PACK * A_COLS * (j + 1)].bitcast(I32),
-                )
-                a_pieces.append(a_piece)
+            block_start = [sum(A_BLOCK_COLS[:blk]) for blk in range(len(A_BLOCK_COLS))]
+            a_pieces = {}
+            for blk, cols in enumerate(A_BLOCK_COLS):
+                for xg in range(X_PASSES):
+                    a_piece = ring.tile([P, cols], U32, align_bytes=64, tag="piece")
+                    nc.sync.dma_start(
+                        out=a_piece[:].bitcast(I32),
+                        in_=Wqa_words[xg]
+                        .rearrange("p n t -> p (n t)")[
+                            :, PACK * block_start[blk] : PACK * (block_start[blk] + cols)
+                        ]
+                        .bitcast(I32),
+                    )
+                    a_pieces[(xg, blk)] = a_piece
 
             b_pieces = [load_b_piece(i) for i in range(B_AHEAD)]
 
@@ -252,18 +259,20 @@ def tile_multiheadlatentattention_pa_k_kernel(
 
             square_sums = once.tile([P, H_PASSES], F32)
 
-            def multiply_piece(j):
+            def multiply_step(j):
                 sorted_banks = []
-                for half in range(A_COLS // BANK):
-                    g = (A_COLS // BANK) * j + half
+                for half in range(STEP_BANKS):
+                    g = STEP_BANKS * j + half
                     plane, plane_col = divmod(BANK * g, A_QUARTER)
+                    blk = max([n for n in range(len(A_BLOCK_COLS)) if block_start[n] <= BANK * g])
+                    block_col = BANK * g - block_start[blk]
                     c_bank = psum_c.tile([P, BANK], F32, tag="c_bank")
                     for xg in range(X_PASSES):
                         nc.tensor.matmul_mx(
                             out=c_bank[:],
                             lhsT=x_codes[:, P * xg : P * (xg + 1)].bitcast(FP8X4),
                             lhsT_scale=x_scales[:, P * xg : P * (xg + 1)],
-                            rhs=a_pieces[j][:, xg, BANK * half : BANK * (half + 1)].bitcast(FP8X4),
+                            rhs=a_pieces[(xg, blk)][:, block_col : block_col + BANK].bitcast(FP8X4),
                             rhs_scale=a_planes[4 * plane : P, xg, plane_col : plane_col + BANK],
                             start=(xg == 0),
                             stop=(xg == X_PASSES - 1),
@@ -282,7 +291,7 @@ def tile_multiheadlatentattention_pa_k_kernel(
                     sorted_banks.append((g, c_sorted))
                 return sorted_banks
 
-            def transpose_piece(sorted_banks):
+            def transpose_step(sorted_banks):
                 for g, c_sorted in sorted_banks:
                     c_t = psum_c.tile([P, PACK, P], F32, tag="transposed")
                     for t in range(PACK):
@@ -294,14 +303,16 @@ def tile_multiheadlatentattention_pa_k_kernel(
                         op=ALU.mult,
                     )
 
-            waiting = multiply_piece(0)
-            b_pieces.append(load_b_piece(B_AHEAD))
-            for j in range(1, A_PIECES):
-                arrived = multiply_piece(j)
-                b_pieces.append(load_b_piece(B_AHEAD + j))
-                transpose_piece(waiting)
+            block_end = [block_start[blk] + cols for blk, cols in enumerate(A_BLOCK_COLS)]
+            waiting = []
+            for j in range(STEPS):
+                arrived = multiply_step(j)
+                if STEP_BANKS * BANK * (j + 1) in block_end:
+                    for xg in range(X_PASSES):
+                        b_pieces.append(load_b_piece(len(b_pieces)))
+                transpose_step(waiting)
                 waiting = arrived
-            transpose_piece(waiting)
+            transpose_step(waiting)
 
             mean_square = once.tile([P, 1], F32)
             nc.vector.reduce_sum(out=mean_square[:], in_=square_sums[:], axis=AXIS.X)

@@ -38,8 +38,8 @@ A_QUARTER = RANK // PLANES
 
 GROUP_HEADS = (8, 6, 2)
 GROUPS = len(GROUP_HEADS)
-WHOLE_ROW_PASSES = 6
-TWO_GROUP_PASSES = 6
+WHOLE_ROW_PASSES = 4
+TWO_GROUP_PASSES = 8
 RING = 12
 B_AHEAD = RING - A_PIECES
 
@@ -372,7 +372,14 @@ def tile_multiheadlatentattention_pa_k_kernel(
                 q_heads = finish.tile([P, heads, D_HEAD], F32, tag="q_heads_%d" % grp)
                 q_flat = q_heads[:].rearrange("p h f -> p (h f)")
                 for n, (start, width) in enumerate(slices[grp]):
-                    nc.scalar.copy(out=q_flat[:, start : start + width], in_=q_banks[grp][n][:])
+                    if n % 2 == 0:
+                        nc.scalar.copy(
+                            out=q_flat[:, start : start + width], in_=q_banks[grp][n][:]
+                        )
+                    else:
+                        nc.vector.tensor_copy(
+                            out=q_flat[:, start : start + width], in_=q_banks[grp][n][:]
+                        )
                 rope = q_heads[:, :, D_NOPE:D_HEAD]
                 pairs = rope.rearrange("p h (i two) -> p h i two", two=2)
                 neighbour = finish.tile([P, heads, 2, D_ROPE // 2], F32, tag="neighbour_%d" % grp)

@@ -30,7 +30,7 @@ X_PASSES = D_MODEL // K_PASS
 H_PASSES = RANK // K_PASS
 
 A_BLOCK_COLS = (3072, 3072, 2048)
-A_PIECES = X_PASSES * len(A_BLOCK_COLS)
+A_PIECES = len(A_BLOCK_COLS)
 STEP_BANKS = 2
 STEPS = RANK // (STEP_BANKS * BANK)
 PLANES = 4
@@ -38,9 +38,11 @@ A_QUARTER = RANK // PLANES
 
 GROUP_HEADS = (8, 6, 2)
 GROUPS = len(GROUP_HEADS)
-WHOLE_ROW_PASSES = 4
-TWO_GROUP_PASSES = 8
-RING = 12
+WHOLE_ROW_PASSES = 6
+TWO_GROUP_PASSES = 6
+PIECE_PASSES = 2
+LAST_GROUP_PIECES = (4, 3, 2, 1)
+RING = 6
 B_AHEAD = RING - A_PIECES
 
 ROUND_MAGIC = 12582912.0
@@ -61,11 +63,15 @@ def moving_slices(cols):
 
 def piece_plan():
     split_from = WHOLE_ROW_PASSES + TWO_GROUP_PASSES
-    plan = [(g, 0, GROUPS) for g in range(WHOLE_ROW_PASSES)]
-    plan += [(g, 0, 2) for g in range(WHOLE_ROW_PASSES, split_from)]
-    plan += [(g, 0, 1) for g in range(split_from, H_PASSES)]
-    plan += [(g, 1, 1) for g in range(split_from, H_PASSES)]
-    plan += [(g, 2, 1) for g in range(WHOLE_ROW_PASSES, H_PASSES)]
+    plan = [(g, PIECE_PASSES, 0, GROUPS) for g in range(0, WHOLE_ROW_PASSES, PIECE_PASSES)]
+    plan += [(g, PIECE_PASSES, 0, 2) for g in range(WHOLE_ROW_PASSES, split_from, PIECE_PASSES)]
+    plan += [(g, PIECE_PASSES, 0, 1) for g in range(split_from, H_PASSES, PIECE_PASSES)]
+    plan += [(g, PIECE_PASSES, 1, 1) for g in range(split_from, H_PASSES, PIECE_PASSES)]
+    g = WHOLE_ROW_PASSES
+    for passes in LAST_GROUP_PIECES:
+        plan.append((g, passes, 2, 1))
+        g += passes
+    assert g == H_PASSES
     return plan
 
 
@@ -89,14 +95,16 @@ def tile_multiheadlatentattention_pa_k_kernel(
         h_scales = keep.tile([P, H_PASSES, P], U8, align_bytes=64)
 
         def load_b_piece(i):
-            g, first_group, groups = plan[i]
+            first_pass, passes, first_group, groups = plan[i]
             first_col = first_head[first_group] * D_HEAD
             cols = sum(GROUP_HEADS[first_group : first_group + groups]) * D_HEAD
-            b_piece = ring.tile([P, cols], U32, align_bytes=64, tag="piece")
+            b_piece = ring.tile([P, passes, cols], U32, align_bytes=64, tag="piece")
             nc.sync.dma_start(
                 out=b_piece[:].bitcast(I32),
-                in_=Wqb_words[g]
-                .rearrange("p n t -> p (n t)")[:, PACK * first_col : PACK * (first_col + cols)]
+                in_=Wqb_words[first_pass : first_pass + passes]
+                .rearrange("g p n t -> p g (n t)")[
+                    :, :, PACK * first_col : PACK * (first_col + cols)
+                ]
                 .bitcast(I32),
             )
             return b_piece
@@ -123,19 +131,17 @@ def tile_multiheadlatentattention_pa_k_kernel(
             )
 
             block_start = [sum(A_BLOCK_COLS[:blk]) for blk in range(len(A_BLOCK_COLS))]
-            a_pieces = {}
+            a_words = Wqa_words.rearrange("g p n t -> p g (n t)")
+            a_pieces = []
             for blk, cols in enumerate(A_BLOCK_COLS):
-                for xg in range(X_PASSES):
-                    a_piece = ring.tile([P, cols], U32, align_bytes=64, tag="piece")
-                    nc.sync.dma_start(
-                        out=a_piece[:].bitcast(I32),
-                        in_=Wqa_words[xg]
-                        .rearrange("p n t -> p (n t)")[
-                            :, PACK * block_start[blk] : PACK * (block_start[blk] + cols)
-                        ]
-                        .bitcast(I32),
-                    )
-                    a_pieces[(xg, blk)] = a_piece
+                a_piece = ring.tile([P, X_PASSES, cols], U32, align_bytes=64, tag="piece")
+                nc.sync.dma_start(
+                    out=a_piece[:].bitcast(I32),
+                    in_=a_words[
+                        :, :, PACK * block_start[blk] : PACK * (block_start[blk] + cols)
+                    ].bitcast(I32),
+                )
+                a_pieces.append(a_piece)
 
             b_pieces = [load_b_piece(i) for i in range(B_AHEAD)]
 
@@ -272,7 +278,7 @@ def tile_multiheadlatentattention_pa_k_kernel(
                             out=c_bank[:],
                             lhsT=x_codes[:, P * xg : P * (xg + 1)].bitcast(FP8X4),
                             lhsT_scale=x_scales[:, P * xg : P * (xg + 1)],
-                            rhs=a_pieces[(xg, blk)][:, block_col : block_col + BANK].bitcast(FP8X4),
+                            rhs=a_pieces[blk][:, xg, block_col : block_col + BANK].bitcast(FP8X4),
                             rhs_scale=a_planes[4 * plane : P, xg, plane_col : plane_col + BANK],
                             start=(xg == 0),
                             stop=(xg == X_PASSES - 1),
@@ -308,8 +314,7 @@ def tile_multiheadlatentattention_pa_k_kernel(
             for j in range(STEPS):
                 arrived = multiply_step(j)
                 if STEP_BANKS * BANK * (j + 1) in block_end:
-                    for xg in range(X_PASSES):
-                        b_pieces.append(load_b_piece(len(b_pieces)))
+                    b_pieces.append(load_b_piece(len(b_pieces)))
                 transpose_step(waiting)
                 waiting = arrived
             transpose_step(waiting)
@@ -431,28 +436,29 @@ def tile_multiheadlatentattention_pa_k_kernel(
                 return q_heads
 
             rotated = []
-            for i, (g, first_group, groups) in enumerate(plan):
-                a, plane = divmod(g, PLANES)
-                for grp in range(first_group, first_group + groups):
-                    group_col = first_head[grp] * D_HEAD
-                    piece_col = group_col - first_head[first_group] * D_HEAD
-                    for q_bank, (start, width) in zip(q_banks[grp], slices[grp]):
-                        nc.tensor.matmul_mx(
-                            out=q_bank[:],
-                            lhsT=h_codes[:, g, :].bitcast(FP8X4),
-                            lhsT_scale=h_scales[:, g, :],
-                            rhs=b_pieces[i][
-                                :, piece_col + start : piece_col + start + width
-                            ].bitcast(FP8X4),
-                            rhs_scale=b_planes[
-                                4 * plane : P, a, group_col + start : group_col + start + width
-                            ],
-                            start=(g == 0),
-                            stop=(g == H_PASSES - 1),
-                        )
+            for i, (first_pass, passes, first_group, groups) in enumerate(plan):
+                for g in range(first_pass, first_pass + passes):
+                    a, plane = divmod(g, PLANES)
+                    for grp in range(first_group, first_group + groups):
+                        group_col = first_head[grp] * D_HEAD
+                        piece_col = group_col - first_head[first_group] * D_HEAD
+                        for q_bank, (start, width) in zip(q_banks[grp], slices[grp]):
+                            nc.tensor.matmul_mx(
+                                out=q_bank[:],
+                                lhsT=h_codes[:, g, :].bitcast(FP8X4),
+                                lhsT_scale=h_scales[:, g, :],
+                                rhs=b_pieces[i][
+                                    :, g - first_pass, piece_col + start : piece_col + start + width
+                                ].bitcast(FP8X4),
+                                rhs_scale=b_planes[
+                                    4 * plane : P, a, group_col + start : group_col + start + width
+                                ],
+                                start=(g == 0),
+                                stop=(g == H_PASSES - 1),
+                            )
                 if i + RING < len(plan):
                     b_pieces.append(load_b_piece(i + RING))
-                if g == H_PASSES - 1:
+                if first_pass + passes == H_PASSES:
                     if first_group == GROUPS - 1:
                         rotated.append(rotate_last_group(first_group))
                     else:

@@ -36,12 +36,13 @@ STEPS = RANK // (STEP_BANKS * BANK)
 PLANES = 4
 A_QUARTER = RANK // PLANES
 
-GROUP_HEADS = (8, 6, 2)
-GROUPS = len(GROUP_HEADS)
+GROUP_COLS = (8 * D_HEAD, 6 * D_HEAD, D_HEAD + D_NOPE, D_ROPE)
+GROUPS = len(GROUP_COLS)
 WHOLE_ROW_PASSES = 6
 TWO_GROUP_PASSES = 6
 PIECE_PASSES = 2
-LAST_GROUP_PIECES = (4, 3, 2, 1)
+SMALL_PAIR_PIECES = (4, 2)
+SMALL_GROUP_PIECES = (3, 1)
 RING = 6
 B_AHEAD = RING - A_PIECES
 
@@ -68,10 +69,16 @@ def piece_plan():
     plan += [(g, PIECE_PASSES, 0, 1) for g in range(split_from, H_PASSES, PIECE_PASSES)]
     plan += [(g, PIECE_PASSES, 1, 1) for g in range(split_from, H_PASSES, PIECE_PASSES)]
     g = WHOLE_ROW_PASSES
-    for passes in LAST_GROUP_PIECES:
-        plan.append((g, passes, 2, 1))
+    for passes in SMALL_PAIR_PIECES:
+        plan.append((g, passes, 2, 2))
         g += passes
-    assert g == H_PASSES
+    assert g == split_from
+    for grp in (2, 3):
+        g = split_from
+        for passes in SMALL_GROUP_PIECES:
+            plan.append((g, passes, grp, 1))
+            g += passes
+        assert g == H_PASSES
     return plan
 
 
@@ -79,7 +86,7 @@ def tile_multiheadlatentattention_pa_k_kernel(
     tc, x, Wqa_words, Wqa_scales, q_a_norm_w, Wqb_words, Wqb_scales, out
 ):
     nc = tc.nc
-    first_head = [sum(GROUP_HEADS[:grp]) for grp in range(GROUPS)]
+    group_start = [sum(GROUP_COLS[:grp]) for grp in range(GROUPS)]
     plan = piece_plan()
 
     with ExitStack() as whole_kernel:
@@ -96,8 +103,8 @@ def tile_multiheadlatentattention_pa_k_kernel(
 
         def load_b_piece(i):
             first_pass, passes, first_group, groups = plan[i]
-            first_col = first_head[first_group] * D_HEAD
-            cols = sum(GROUP_HEADS[first_group : first_group + groups]) * D_HEAD
+            first_col = group_start[first_group]
+            cols = sum(GROUP_COLS[first_group : first_group + groups])
             b_piece = ring.tile([P, passes, cols], U32, align_bytes=64, tag="piece")
             nc.sync.dma_start(
                 out=b_piece[:].bitcast(I32),
@@ -355,7 +362,7 @@ def tile_multiheadlatentattention_pa_k_kernel(
                     in_=h_grouped[:].rearrange("p k t -> p (k t)"),
                 )
 
-            slices = [moving_slices(heads * D_HEAD) for heads in GROUP_HEADS]
+            slices = [moving_slices(cols) for cols in GROUP_COLS]
             q_banks = []
             for grp in range(GROUPS):
                 group_banks = []
@@ -373,7 +380,7 @@ def tile_multiheadlatentattention_pa_k_kernel(
                 )
 
             def rotate_group(grp):
-                heads = GROUP_HEADS[grp]
+                heads = GROUP_COLS[grp] // D_HEAD
                 q_heads = finish.tile([P, heads, D_HEAD], F32, tag="q_heads_%d" % grp)
                 q_flat = q_heads[:].rearrange("p h f -> p (h f)")
                 for n, (start, width) in enumerate(slices[grp]):
@@ -407,41 +414,39 @@ def tile_multiheadlatentattention_pa_k_kernel(
                 add_neighbours(q_heads, turned[:], neighbour)
                 return q_heads
 
-            def rotate_last_group(grp):
-                q_heads = finish.tile([P, 2, D_HEAD], F32, tag="q_heads_%d" % grp)
-                q_flat = q_heads[:].rearrange("p h f -> p (h f)")
-                neighbour = finish.tile([P, 2, 2, D_ROPE // 2], F32, tag="neighbour_%d" % grp)
-                wide_bank, rope_bank = q_banks[grp]
-                nc.vector.tensor_tensor(
-                    out=q_flat[:, 0 : D_NOPE + D_HEAD], in0=wide_bank[:], in1=cos_wide[:], op=ALU.mult
+            def rotate_bank(grp, factors, first):
+                bank = q_banks[grp][0]
+                turned = finish.tile([P, GROUP_COLS[grp]], F32, tag="turned_%d" % grp)
+                neighbour = finish.tile([P, 2, D_ROPE // 2], F32, tag="neighbour_%d" % grp)
+                nc.vector.tensor_tensor(out=turned[:], in0=bank[:], in1=factors, op=ALU.mult)
+                bank_pairs = bank[:, first : first + D_ROPE].rearrange(
+                    "p (i two) -> p i two", two=2
                 )
-                bank_ropes = (wide_bank[:, D_NOPE:D_HEAD], rope_bank[:])
-                for head in range(2):
-                    if head == 1:
-                        nc.vector.tensor_tensor(
-                            out=q_heads[:, 1, D_NOPE:D_HEAD],
-                            in0=rope_bank[:],
-                            in1=cos_table,
-                            op=ALU.mult,
-                        )
-                    bank_pairs = bank_ropes[head].rearrange("p (i two) -> p i two", two=2)
-                    for two in range(2):
-                        nc.vector.tensor_tensor(
-                            out=neighbour[:, head, two, :],
-                            in0=bank_pairs[:, :, 1 - two],
-                            in1=sin_planes[:, two, :],
-                            op=ALU.mult,
-                        )
-                add_neighbours(q_heads, q_heads[:, :, D_NOPE:D_HEAD], neighbour)
-                return q_heads
+                for two in range(2):
+                    nc.vector.tensor_tensor(
+                        out=neighbour[:, two, :],
+                        in0=bank_pairs[:, :, 1 - two],
+                        in1=sin_planes[:, two, :],
+                        op=ALU.mult,
+                    )
+                turned_pairs = turned[:, first : first + D_ROPE].rearrange(
+                    "p (i two) -> p i two", two=2
+                )
+                nc.vector.tensor_tensor(
+                    out=turned_pairs,
+                    in0=turned_pairs,
+                    in1=neighbour[:].rearrange("p two i -> p i two"),
+                    op=ALU.add,
+                )
+                return turned
 
             rotated = []
             for i, (first_pass, passes, first_group, groups) in enumerate(plan):
                 for g in range(first_pass, first_pass + passes):
                     a, plane = divmod(g, PLANES)
                     for grp in range(first_group, first_group + groups):
-                        group_col = first_head[grp] * D_HEAD
-                        piece_col = group_col - first_head[first_group] * D_HEAD
+                        group_col = group_start[grp]
+                        piece_col = group_col - group_start[first_group]
                         for q_bank, (start, width) in zip(q_banks[grp], slices[grp]):
                             nc.tensor.matmul_mx(
                                 out=q_bank[:],
@@ -459,16 +464,28 @@ def tile_multiheadlatentattention_pa_k_kernel(
                 if i + RING < len(plan):
                     b_pieces.append(load_b_piece(i + RING))
                 if first_pass + passes == H_PASSES:
-                    if first_group == GROUPS - 1:
-                        rotated.append(rotate_last_group(first_group))
+                    if first_group == 2:
+                        rotated.append(rotate_bank(2, cos_wide[:], D_NOPE))
+                    elif first_group == 3:
+                        rotated.append(rotate_bank(3, cos_table, 0))
                     else:
                         rotated.append(rotate_group(first_group))
 
-            for grp in range(GROUPS):
+            for grp in range(2):
+                first_head = group_start[grp] // D_HEAD
+                heads = GROUP_COLS[grp] // D_HEAD
                 for b in range(BATCH):
                     nc.sync.dma_start(
-                        out=out[b, first_head[grp] : first_head[grp] + GROUP_HEADS[grp]].rearrange(
-                            "h s f -> s h f"
-                        ),
+                        out=out[b, first_head : first_head + heads].rearrange("h s f -> s h f"),
                         in_=rotated[grp][b:P:BATCH, :, :],
                     )
+            for b in range(BATCH):
+                nc.sync.dma_start(out=out[b, HEADS - 2], in_=rotated[2][b:P:BATCH, 0:D_HEAD])
+                nc.sync.dma_start(
+                    out=out[b, HEADS - 1, :, 0:D_NOPE],
+                    in_=rotated[2][b:P:BATCH, D_HEAD : D_HEAD + D_NOPE],
+                )
+            for b in range(BATCH):
+                nc.sync.dma_start(
+                    out=out[b, HEADS - 1, :, D_NOPE:D_HEAD], in_=rotated[3][b:P:BATCH, :]
+                )

@@ -38,10 +38,10 @@ A_QUARTER = RANK // PLANES
 
 GROUP_COLS = (8 * D_HEAD, 6 * D_HEAD, D_HEAD + D_NOPE, D_ROPE)
 GROUPS = len(GROUP_COLS)
-WHOLE_ROW_PASSES = 6
-TWO_GROUP_PASSES = 6
+WHOLE_ROW_PASSES = 4
+TWO_GROUP_PASSES = 8
 PIECE_PASSES = 2
-SMALL_PAIR_PIECES = (4, 2)
+SMALL_PAIR_PIECES = (4, 4)
 SMALL_GROUP_PIECES = (3, 1)
 RING = 6
 B_AHEAD = RING - A_PIECES

import math
from contextlib import ExitStack

import concourse.masks as masks
import concourse.mybir as mybir

F32 = mybir.dt.float32
BF16 = mybir.dt.bfloat16
I32 = mybir.dt.int32
U32 = mybir.dt.uint32
U8 = mybir.dt.uint8
FP8X4 = mybir.dt.float8_e4m3fn_x4
ALU = mybir.AluOpType
ACT = mybir.ActivationFunctionType
AXIS = mybir.AxisListType

P = 128
PACK = 4
K_PASS = P * PACK
BANK = 512

BATCH, SEQ, D_MODEL = 2, 64, 1024
RANK = 8192
HEADS, D_NOPE, D_ROPE = 16, 64, 128
D_HEAD = D_NOPE + D_ROPE
THETA = 10000.0
EPS = 1e-6

X_PASSES = D_MODEL // K_PASS
H_PASSES = RANK // K_PASS

A_BLOCK_COLS = (3072, 3072, 2048)
A_PIECES = len(A_BLOCK_COLS)
STEP_BANKS = 2
STEPS = RANK // (STEP_BANKS * BANK)
PLANES = 4
A_QUARTER = RANK // PLANES

GROUP_COLS = (8 * D_HEAD, 6 * D_HEAD, D_HEAD + D_NOPE, D_ROPE)
GROUPS = len(GROUP_COLS)
WHOLE_ROW_PASSES = 4
TWO_GROUP_PASSES = 8
PIECE_PASSES = 2
SMALL_PAIR_PIECES = (4, 4)
SMALL_GROUP_PIECES = (3, 1)
RING = 6
B_AHEAD = RING - A_PIECES

ROUND_MAGIC = 12582912.0

FLOPS = 2 * P * (D_MODEL * RANK + RANK * HEADS * D_HEAD)


def moving_slices(cols):
    slices = []
    start = 0
    for width in (BANK, 256, 128):
        while cols - start >= width:
            slices.append((start, width))
            start += width
    assert start == cols
    return slices


def piece_plan():
    split_from = WHOLE_ROW_PASSES + TWO_GROUP_PASSES
    plan = [(g, PIECE_PASSES, 0, GROUPS) for g in range(0, WHOLE_ROW_PASSES, PIECE_PASSES)]
    plan += [(g, PIECE_PASSES, 0, 2) for g in range(WHOLE_ROW_PASSES, split_from, PIECE_PASSES)]
    plan += [(g, PIECE_PASSES, 0, 1) for g in range(split_from, H_PASSES, PIECE_PASSES)]
    plan += [(g, PIECE_PASSES, 1, 1) for g in range(split_from, H_PASSES, PIECE_PASSES)]
    g = WHOLE_ROW_PASSES
    for passes in SMALL_PAIR_PIECES:
        plan.append((g, passes, 2, 2))
        g += passes
    assert g == split_from
    for grp in (2, 3):
        g = split_from
        for passes in SMALL_GROUP_PIECES:
            plan.append((g, passes, grp, 1))
            g += passes
        assert g == H_PASSES
    return plan


def tile_multiheadlatentattention_pa_k_kernel(
    tc, x, Wqa_words, Wqa_scales, q_a_norm_w, Wqb_words, Wqb_scales, out
):
    nc = tc.nc
    group_start = [sum(GROUP_COLS[:grp]) for grp in range(GROUPS)]
    plan = piece_plan()

    with ExitStack() as whole_kernel:
        keep = whole_kernel.enter_context(tc.tile_pool(name="keep", bufs=1))
        ring = whole_kernel.enter_context(tc.tile_pool(name="ring", bufs=RING))

        c_gain = keep.tile([P, H_PASSES, P, PACK], F32)
        rstd_all = keep.tile([P, P], F32)
        table = keep.tile([P, 2 * D_ROPE], F32)
        cos_wide = keep.tile([P, D_NOPE + D_HEAD], F32)
        b_planes = keep.tile([P, H_PASSES // PLANES, HEADS * D_HEAD], U8, align_bytes=64)
        h_codes = keep.tile([P, H_PASSES, P], U32, align_bytes=64)
        h_scales = keep.tile([P, H_PASSES, P], U8, align_bytes=64)

        def load_b_piece(i):
            first_pass, passes, first_group, groups = plan[i]
            first_col = group_start[first_group]
            cols = sum(GROUP_COLS[first_group : first_group + groups])
            b_piece = ring.tile([P, passes, cols], U32, align_bytes=64, tag="piece")
            nc.sync.dma_start(
                out=b_piece[:].bitcast(I32),
                in_=Wqb_words[first_pass : first_pass + passes]
                .rearrange("g p n t -> p g (n t)")[
                    :, :, PACK * first_col : PACK * (first_col + cols)
                ]
                .bitcast(I32),
            )
            return b_piece

        with ExitStack() as first_matmul:
            once = first_matmul.enter_context(tc.tile_pool(name="once", bufs=1))
            stage_c = first_matmul.enter_context(tc.tile_pool(name="stage_c", bufs=4))
            psum_c = first_matmul.enter_context(tc.psum_pool(name="psum_c", bufs=4))

            a_planes = once.tile([P, X_PASSES, A_QUARTER], U8, align_bytes=64)
            gain_rows = once.tile([P, K_PASS], BF16)
            nc.vector.memset(a_planes[:].rearrange("p g n -> p (g n)").bitcast(I32), 0)
            nc.vector.memset(gain_rows[:], 0.0)
            nc.vector.memset(cos_wide[:], 1.0)
            nc.vector.memset(b_planes[:].rearrange("p a n -> p (a n)").bitcast(I32), 0)

            x_sb = once.tile([P, D_MODEL], BF16)
            for b in range(BATCH):
                nc.scalar.dma_start(out=x_sb[b:P:BATCH, :], in_=x[b])

            nc.scalar.dma_start(
                out=gain_rows[0:H_PASSES, :],
                in_=q_a_norm_w.rearrange("(g k) -> g k", g=H_PASSES),
            )

            block_start = [sum(A_BLOCK_COLS[:blk]) for blk in range(len(A_BLOCK_COLS))]
            a_words = Wqa_words.rearrange("g p n t -> p g (n t)")
            a_pieces = []
            for blk, cols in enumerate(A_BLOCK_COLS):
                a_piece = ring.tile([P, X_PASSES, cols], U32, align_bytes=64, tag="piece")
                nc.sync.dma_start(
                    out=a_piece[:].bitcast(I32),
                    in_=a_words[
                        :, :, PACK * block_start[blk] : PACK * (block_start[blk] + cols)
                    ].bitcast(I32),
                )
                a_pieces.append(a_piece)

            b_pieces = [load_b_piece(i) for i in range(B_AHEAD)]

            ident = once.tile([P, P], F32)
            masks.make_identity(nc, ident[:])

            for g in range(X_PASSES):
                for quad in range(4):
                    nc.gpsimd.dma_start(
                        out=a_planes[32 * quad : 32 * quad + 16, g, :].bitcast(F32),
                        in_=Wqa_scales[g, 4 * quad : 4 * quad + 4, :]
                        .rearrange("r (j n) -> j r n", j=PLANES)
                        .bitcast(F32),
                    )

            angle_index = once.tile([P, 2 * D_ROPE], I32)
            nc.gpsimd.iota(
                angle_index[:, 0:D_ROPE], pattern=[[0, 2], [1, 64]], base=0, channel_multiplier=0
            )
            nc.gpsimd.iota(
                angle_index[:, D_ROPE : 2 * D_ROPE],
                pattern=[[1, 2], [0, 2], [2, 32]],
                base=0,
                channel_multiplier=0,
            )
            partition_index = once.tile([P, 1], I32)
            nc.gpsimd.iota(partition_index[:], pattern=[[0, 1]], base=0, channel_multiplier=1)

            for a in range(H_PASSES // PLANES):
                for quad in range(4):
                    nc.gpsimd.dma_start(
                        out=b_planes[32 * quad : 32 * quad + 16, a, :].bitcast(F32),
                        in_=Wqb_scales[
                            PLANES * a : PLANES * (a + 1), 4 * quad : 4 * quad + 4, :
                        ].bitcast(F32),
                    )

            position_int = once.tile([P, 1], I32)
            nc.vector.tensor_single_scalar(
                out=position_int[:], in_=partition_index[:], scalar=1, op=ALU.arith_shift_right
            )
            position = once.tile([P, 1], F32)
            nc.vector.tensor_copy(out=position[:], in_=position_int[:])

            inv_freq = once.tile([P, 2 * D_ROPE], F32)
            nc.vector.tensor_copy(out=inv_freq[:], in_=angle_index[:])
            nc.scalar.activation(
                out=inv_freq[:], in_=inv_freq[:], func=ACT.Exp, scale=-math.log(THETA) / 64.0
            )
            angle = once.tile([P, 2 * D_ROPE], F32)
            nc.vector.tensor_scalar(
                out=angle[:, 0:D_ROPE],
                in0=inv_freq[:, 0:D_ROPE],
                scalar1=position[:, 0:1],
                scalar2=math.pi / 2.0,
                op0=ALU.mult,
                op1=ALU.add,
            )
            nc.vector.tensor_scalar_mul(
                out=angle[:, D_ROPE : 2 * D_ROPE],
                in0=inv_freq[:, D_ROPE : 2 * D_ROPE],
                scalar1=position[:, 0:1],
            )
            whole_turns = once.tile([P, 2 * D_ROPE], F32)
            nc.vector.tensor_scalar(
                out=whole_turns[:],
                in0=angle[:],
                scalar1=1.0 / (2.0 * math.pi),
                scalar2=ROUND_MAGIC,
                op0=ALU.mult,
                op1=ALU.add,
            )
            nc.vector.tensor_scalar(
                out=whole_turns[:],
                in0=whole_turns[:],
                scalar1=ROUND_MAGIC,
                scalar2=2.0 * math.pi,
                op0=ALU.subtract,
                op1=ALU.mult,
            )
            nc.vector.tensor_sub(out=angle[:], in0=angle[:], in1=whole_turns[:])
            nc.scalar.activation(out=table[:], in_=angle[:], func=ACT.Sin)
            cos_table = table[:, 0:D_ROPE]
            nc.vector.tensor_copy(out=cos_wide[:, D_NOPE:D_HEAD], in_=cos_table)
            sin_planes = table[:, D_ROPE : 2 * D_ROPE].rearrange("p (two i) -> p two i", two=2)
            nc.vector.tensor_scalar_mul(
                out=sin_planes[:, 0, :], in0=sin_planes[:, 0, :], scalar1=-1.0
            )

            x_words = x_sb[:].bitcast(F32)
            x_t = psum_c.tile([P, X_PASSES, 2, P], F32, tag="transposed")
            for g in range(X_PASSES):
                for u in range(2):
                    nc.tensor.transpose(
                        x_t[:, g, u, :],
                        x_words[:, 256 * g + u : 256 * (g + 1) : 2],
                        ident[:],
                    )
            x_grouped = once.tile([P, X_PASSES * P * PACK], BF16, align_bytes=64)
            nc.vector.tensor_copy(
                out=x_grouped[:].bitcast(F32).rearrange("p (g k u) -> p g k u", g=X_PASSES, u=2),
                in_=x_t[:].rearrange("p g u k -> p g k u"),
            )
            x_codes = once.tile([P, X_PASSES * P], U32, align_bytes=64)
            x_scales = once.tile([P, X_PASSES * P], U8, align_bytes=64)
            nc.vector.quantize_mx(
                out=x_codes[:].bitcast(FP8X4), scales=x_scales[:], in_=x_grouped[:]
            )

            gain_sorted = once.tile([P, PACK, P], F32)
            nc.vector.tensor_copy(
                out=gain_sorted[:], in_=gain_rows[:].rearrange("g (p t) -> g t p", t=PACK)
            )
            gain_t = psum_c.tile([P, PACK, P], F32, tag="transposed")
            for t in range(PACK):
                nc.tensor.transpose(gain_t[:, t, :], gain_sorted[:, t, :], ident[:])
            gain = once.tile([P, H_PASSES, PACK], F32)
            nc.vector.tensor_copy(
                out=gain[:], in_=gain_t[:, :, 0:H_PASSES].rearrange("p t g -> p g t")
            )

            square_sums = once.tile([P, H_PASSES], F32)

            def multiply_step(j):
                sorted_banks = []
                for half in range(STEP_BANKS):
                    g = STEP_BANKS * j + half
                    plane, plane_col = divmod(BANK * g, A_QUARTER)
                    blk = max([n for n in range(len(A_BLOCK_COLS)) if block_start[n] <= BANK * g])
                    block_col = BANK * g - block_start[blk]
                    c_bank = psum_c.tile([P, BANK], F32, tag="c_bank")
                    for xg in range(X_PASSES):
                        nc.tensor.matmul_mx(
                            out=c_bank[:],
                            lhsT=x_codes[:, P * xg : P * (xg + 1)].bitcast(FP8X4),
                            lhsT_scale=x_scales[:, P * xg : P * (xg + 1)],
                            rhs=a_pieces[blk][:, xg, block_col : block_col + BANK].bitcast(FP8X4),
                            rhs_scale=a_planes[4 * plane : P, xg, plane_col : plane_col + BANK],
                            start=(xg == 0),
                            stop=(xg == X_PASSES - 1),
                        )
                    c_sorted = stage_c.tile([P, PACK, P], F32)
                    nc.scalar.copy(
                        out=c_sorted[:], in_=c_bank[:].rearrange("k (p t) -> k t p", t=PACK)
                    )
                    squares = stage_c.tile([P, BANK], BF16, bufs=2)
                    nc.scalar.activation(
                        out=squares[:],
                        in_=c_bank[:],
                        func=ACT.Square,
                        accum_out=square_sums[:, g : g + 1],
                    )
                    sorted_banks.append((g, c_sorted))
                return sorted_banks

            def transpose_step(sorted_banks):
                for g, c_sorted in sorted_banks:
                    c_t = psum_c.tile([P, PACK, P], F32, tag="transposed")
                    for t in range(PACK):
                        nc.tensor.transpose(c_t[:, t, :], c_sorted[:, t, :], ident[:])
                    nc.vector.tensor_tensor(
                        out=c_gain[:, g, :, :],
                        in0=c_t[:].rearrange("p t k -> p k t"),
                        in1=gain[:, g, :].unsqueeze(1).to_broadcast([P, P, PACK]),
                        op=ALU.mult,
                    )

            block_end = [block_start[blk] + cols for blk, cols in enumerate(A_BLOCK_COLS)]
            waiting = []
            for j in range(STEPS):
                arrived = multiply_step(j)
                if STEP_BANKS * BANK * (j + 1) in block_end:
                    b_pieces.append(load_b_piece(len(b_pieces)))
                transpose_step(waiting)
                waiting = arrived
            transpose_step(waiting)

            mean_square = once.tile([P, 1], F32)
            nc.vector.reduce_sum(out=mean_square[:], in_=square_sums[:], axis=AXIS.X)
            nc.vector.tensor_scalar(
                out=mean_square[:],
                in0=mean_square[:],
                scalar1=1.0 / RANK,
                scalar2=EPS,
                op0=ALU.mult,
                op1=ALU.add,
            )
            rstd = once.tile([P, 1], F32)
            nc.scalar.sqrt(out=rstd[:], in_=mean_square[:])
            nc.vector.reciprocal(out=rstd[:], in_=rstd[:])
            rstd_t = psum_c.tile([P, P], F32, tag="transposed")
            nc.tensor.transpose(rstd_t[:], rstd[:, 0:1].to_broadcast([P, P]), ident[:])
            nc.vector.tensor_copy(out=rstd_all[:], in_=rstd_t[:])

        with ExitStack() as second_matmul:
            stage_h = second_matmul.enter_context(tc.tile_pool(name="stage_h", bufs=4))
            finish = second_matmul.enter_context(tc.tile_pool(name="finish", bufs=1))
            psum_q = second_matmul.enter_context(tc.psum_pool(name="psum_q", bufs=1))

            for g in range(H_PASSES):
                h_grouped = stage_h.tile([P, P, PACK], BF16, align_bytes=64)
                nc.vector.tensor_tensor(
                    out=h_grouped[:],
                    in0=c_gain[:, g, :, :],
                    in1=rstd_all[:].unsqueeze(2).to_broadcast([P, P, PACK]),
                    op=ALU.mult,
                )
                nc.vector.quantize_mx(
                    out=h_codes[:, g, :].bitcast(FP8X4),
                    scales=h_scales[:, g, :],
                    in_=h_grouped[:].rearrange("p k t -> p (k t)"),
                )

            slices = [moving_slices(cols) for cols in GROUP_COLS]
            q_banks = []
            for grp in range(GROUPS):
                group_banks = []
                for n, (start, width) in enumerate(slices[grp]):
                    q_bank = psum_q.tile([P, width], F32, tag="q_bank_%d_%d" % (grp, n))
                    group_banks.append(q_bank)
                q_banks.append(group_banks)

            def add_neighbours(q_heads, turned, neighbour):
                nc.vector.tensor_tensor(
                    out=q_heads[:, :, D_NOPE:D_HEAD].rearrange("p h (i two) -> p h i two", two=2),
                    in0=turned.rearrange("p h (i two) -> p h i two", two=2),
                    in1=neighbour[:].rearrange("p h two i -> p h i two"),
                    op=ALU.add,
                )

            def rotate_group(grp):
                heads = GROUP_COLS[grp] // D_HEAD
                q_heads = finish.tile([P, heads, D_HEAD], F32, tag="q_heads_%d" % grp)
                q_flat = q_heads[:].rearrange("p h f -> p (h f)")
                for n, (start, width) in enumerate(slices[grp]):
                    if n % 2 == 0:
                        nc.scalar.copy(
                            out=q_flat[:, start : start + width], in_=q_banks[grp][n][:]
                        )
                    else:
                        nc.vector.tensor_copy(
                            out=q_flat[:, start : start + width], in_=q_banks[grp][n][:]
                        )
                rope = q_heads[:, :, D_NOPE:D_HEAD]
                pairs = rope.rearrange("p h (i two) -> p h i two", two=2)
                neighbour = finish.tile([P, heads, 2, D_ROPE // 2], F32, tag="neighbour_%d" % grp)
                turned = finish.tile([P, heads, D_ROPE], F32, tag="turned_%d" % grp)
                nc.vector.tensor_tensor(
                    out=turned[:],
                    in0=rope,
                    in1=cos_table.unsqueeze(1).to_broadcast([P, heads, D_ROPE]),
                    op=ALU.mult,
                )
                for two in range(2):
                    nc.vector.tensor_tensor(
                        out=neighbour[:, :, two, :],
                        in0=pairs[:, :, :, 1 - two],
                        in1=sin_planes[:, two, :]
                        .unsqueeze(1)
                        .to_broadcast([P, heads, D_ROPE // 2]),
                        op=ALU.mult,
                    )
                add_neighbours(q_heads, turned[:], neighbour)
                return q_heads

            def rotate_bank(grp, factors, first):
                bank = q_banks[grp][0]
                turned = finish.tile([P, GROUP_COLS[grp]], F32, tag="turned_%d" % grp)
                neighbour = finish.tile([P, 2, D_ROPE // 2], F32, tag="neighbour_%d" % grp)
                nc.vector.tensor_tensor(out=turned[:], in0=bank[:], in1=factors, op=ALU.mult)
                bank_pairs = bank[:, first : first + D_ROPE].rearrange(
                    "p (i two) -> p i two", two=2
                )
                for two in range(2):
                    nc.vector.tensor_tensor(
                        out=neighbour[:, two, :],
                        in0=bank_pairs[:, :, 1 - two],
                        in1=sin_planes[:, two, :],
                        op=ALU.mult,
                    )
                turned_pairs = turned[:, first : first + D_ROPE].rearrange(
                    "p (i two) -> p i two", two=2
                )
                nc.vector.tensor_tensor(
                    out=turned_pairs,
                    in0=turned_pairs,
                    in1=neighbour[:].rearrange("p two i -> p i two"),
                    op=ALU.add,
                )
                return turned

            rotated = []
            for i, (first_pass, passes, first_group, groups) in enumerate(plan):
                for g in range(first_pass, first_pass + passes):
                    a, plane = divmod(g, PLANES)
                    for grp in range(first_group, first_group + groups):
                        group_col = group_start[grp]
                        piece_col = group_col - group_start[first_group]
                        for q_bank, (start, width) in zip(q_banks[grp], slices[grp]):
                            nc.tensor.matmul_mx(
                                out=q_bank[:],
                                lhsT=h_codes[:, g, :].bitcast(FP8X4),
                                lhsT_scale=h_scales[:, g, :],
                                rhs=b_pieces[i][
                                    :, g - first_pass, piece_col + start : piece_col + start + width
                                ].bitcast(FP8X4),
                                rhs_scale=b_planes[
                                    4 * plane : P, a, group_col + start : group_col + start + width
                                ],
                                start=(g == 0),
                                stop=(g == H_PASSES - 1),
                            )
                if i + RING < len(plan):
                    b_pieces.append(load_b_piece(i + RING))
                if first_pass + passes == H_PASSES:
                    if first_group == 2:
                        rotated.append(rotate_bank(2, cos_wide[:], D_NOPE))
                    elif first_group == 3:
                        rotated.append(rotate_bank(3, cos_table, 0))
                    else:
                        rotated.append(rotate_group(first_group))

            for grp in range(2):
                first_head = group_start[grp] // D_HEAD
                heads = GROUP_COLS[grp] // D_HEAD
                for b in range(BATCH):
                    nc.sync.dma_start(
                        out=out[b, first_head : first_head + heads].rearrange("h s f -> s h f"),
                        in_=rotated[grp][b:P:BATCH, :, :],
                    )
            for b in range(BATCH):
                nc.sync.dma_start(out=out[b, HEADS - 2], in_=rotated[2][b:P:BATCH, 0:D_HEAD])
                nc.sync.dma_start(
                    out=out[b, HEADS - 1, :, 0:D_NOPE],
                    in_=rotated[2][b:P:BATCH, D_HEAD : D_HEAD + D_NOPE],
                )
            for b in range(BATCH):
                nc.sync.dma_start(
                    out=out[b, HEADS - 1, :, D_NOPE:D_HEAD], in_=rotated[3][b:P:BATCH, :]
                )
